import numpy as np
import ml_dtypes


def mxq(x, axis, fmt="e4m3"):
    dtype, down = {"e4m3": (ml_dtypes.float8_e4m3fn, 7), "e5m2": (ml_dtypes.float8_e5m2, 14)}[fmt]
    v = np.moveaxis(np.asarray(x, np.float32).astype(ml_dtypes.bfloat16).astype(np.float64), axis, -1)
    blocks = v.reshape(v.shape[:-1] + (-1, 32))
    amax = np.abs(blocks).max(-1, keepdims=True)
    byte = np.maximum(np.where(amax > 0, np.frexp(amax)[1] - 1 + 127, 0) - down, 1)
    scale = np.exp2(byte - 127.0)
    codes = (blocks / scale).astype(np.float32).astype(dtype).astype(np.float64)
    return np.moveaxis((codes * scale).reshape(v.shape), -1, axis)


WIDE = False


def mx_kscale(k):
    if not WIDE:
        return np.ones(k)
    levels = np.array([10, -10, 5, -5, 0])
    a = np.random.permutation(np.resize(levels, k // 512 * 4)).reshape(k // 512, 4)
    idx = np.arange(k)
    return np.exp2(a[idx // 512, idx % 128 // 32])


BF16 = ml_dtypes.bfloat16


def bf(x):
    return np.asarray(x, np.float32).astype(BF16)


def f64(x):
    return np.asarray(x).astype(np.float64)


E2M1 = np.array([0.0, 0.5, 1.0, 1.5, 2.0, 3.0, 4.0, 6.0, -0.0, -0.5, -1.0, -1.5, -2.0, -3.0, -4.0, -6.0])


def pack_weight(w, fmt):
    k, n = w.shape
    w = f64(bf(w)).reshape(k // 32, 32, n)
    amax = np.abs(w).max(1)
    if fmt == "e4m3":
        byte = np.frexp(amax)[1] - 1 + 127 - 7
    else:
        mant, ex = np.frexp(amax / 6.0)
        byte = np.where(mant > 0.5, ex, ex - 1) + 127
    byte = np.clip(np.where(amax > 0, byte, 1), 1, 254)
    scaled = (w * np.exp2(127.0 - byte)[:, None, :]).reshape(k, n).astype(np.float32)
    by_word = np.ascontiguousarray(scaled.reshape(k // 512, 128, 4, n).transpose(0, 1, 3, 2))
    if fmt == "e4m3":
        words = by_word.astype(ml_dtypes.float8_e4m3fn).view(np.uint8)
    else:
        c = by_word.astype(ml_dtypes.float4_e2m1fn).view(np.uint8) & 0xF
        words = c[..., 0::2] | (c[..., 1::2] << 4)
    return np.ascontiguousarray(words), np.ascontiguousarray(byte.astype(np.uint8).reshape(k // 512, 16, n))


def unpack_weight(words, scales, fmt):
    g, p, n, _ = words.shape
    if fmt == "e4m3":
        vals = np.ascontiguousarray(words).view(ml_dtypes.float8_e4m3fn).astype(np.float64)
    else:
        nib = np.empty((g, p, n, 4), np.uint8)
        nib[..., 0::2] = words & 0xF
        nib[..., 1::2] = words >> 4
        vals = E2M1[nib]
    vals = vals * np.repeat(np.exp2(scales.astype(np.float64) - 127.0), 8, axis=1)[..., None]
    return vals.transpose(0, 1, 3, 2).reshape(g * 512, n)

def pack4(w):
    words, scales = pack_weight(w, "e2m1")
    return words.reshape(words.shape[0], 128, -1), scales


def unpack4(words, scales):
    return unpack_weight(words.reshape(words.shape[0], 128, -1, 2), scales, "e2m1")


B, N, C, H, REG, QKV, LAYERS, PAIR = 1, 1024, 1024, 8, 5, 3, 12, 2
D = C // H


def setup_inputs():
    s = mx_kscale(C)
    w = np.random.standard_normal((C, QKV * C)) * 1.5 / np.sqrt(C)
    m = np.random.standard_normal(C)
    al = np.random.standard_normal((B, N, 1))
    x = np.random.standard_normal((B, N, C)) + al * m
    gain = np.exp2(np.random.uniform(-1.0, 1.0, (H, 1)))
    g = ((m[:, None] * w[:, :C]).sum(0).reshape(H, D) + np.random.standard_normal((H, D))) * gain
    words, scales = pack4(w / s[:, None])
    return {"x": bf(x * s), "W_qkv_words": words, "W_qkv_scales": scales, "q_g": bf(g)}


def reference(x, W_qkv_words, W_qkv_scales, q_g):
    qkv = (mxq(f64(x), 2, "e4m3") @ unpack4(W_qkv_words, W_qkv_scales)).reshape(B, N, QKV, H, D)
    q, k, v = qkv[:, :, 0], qkv[:, :, 1], qkv[:, :, 2]
    q_pure = q[:, REG:]
    q_n = q_pure / np.sqrt((q_pure ** 2).sum(-1, keepdims=True))
    g = f64(q_g)
    qg_n = g / np.sqrt((g ** 2).sum(-1, keepdims=True))
    sim = (qg_n[None, None] * q_n).sum(-1).mean(-1)
    return q, k, v, sim

@@ -1,0 +1,208 @@
+from contextlib import ExitStack
+
+import concourse.masks as masks
+import concourse.mybir as mybir
+
+F32 = mybir.dt.float32
+BF16 = mybir.dt.bfloat16
+I32 = mybir.dt.int32
+U32 = mybir.dt.uint32
+U8 = mybir.dt.uint8
+FP8X4 = mybir.dt.float8_e4m3fn_x4
+FP4X4 = mybir.dt.float4_e2m1fn_x4
+ACT = mybir.ActivationFunctionType
+ALU = mybir.AluOpType
+AXIS = mybir.AxisListType
+
+P = 128
+TOKENS = 1024
+K = 1024
+HEADS = 8
+HEAD_DIM = 128
+WIDTH = HEADS * HEAD_DIM
+REGISTER_TOKENS = 5
+TOKEN_TILES = TOKENS // P
+PASSES = K // (4 * P)
+BANK = 512
+BANKS_PER_OUTPUT = WIDTH // BANK
+QKV = 3
+
+FLOPS = 2 * TOKENS * K * QKV * WIDTH
+
+
+def tile_memeffattention_pa_kernel(tc, x, w_words, w_scales, q_g, q_out, k_out, v_out, sim_out):
+    nc = tc.nc
+    x_tiles = x.rearrange("b (m p) k -> (b m) p k", p=P)
+    q_tiles = q_out.rearrange("b (m p) h d -> (b m) p (h d)", p=P)
+    k_tiles = k_out.rearrange("b (m p) h d -> (b m) p (h d)", p=P)
+    v_tiles = v_out.rearrange("b (m p) h d -> (b m) p (h d)", p=P)
+
+    with ExitStack() as ctx:
+        keep = ctx.enter_context(tc.tile_pool(name="keep", bufs=1))
+        regroup = ctx.enter_context(tc.tile_pool(name="regroup", bufs=2))
+        results = ctx.enter_context(tc.tile_pool(name="results", bufs=3))
+        unread = ctx.enter_context(tc.tile_pool(name="unread", bufs=2))
+        product_banks = ctx.enter_context(tc.psum_pool(name="product_banks", bufs=6))
+        side_banks = ctx.enter_context(tc.psum_pool(name="side_banks", bufs=2))
+        ctx.enter_context(tc.manual_schedule())
+
+        x_sb = keep.tile([P, TOKEN_TILES, K], BF16)
+        x_codes = keep.tile([P, TOKEN_TILES, PASSES * P], U32, align_bytes=64)
+        x_scales = keep.tile([P, TOKEN_TILES, PASSES * P], U8, align_bytes=64)
+        w_sb = keep.tile([P, PASSES, 2 * QKV * WIDTH], U8, align_bytes=64)
+        w_planes = keep.tile([P, PASSES, QKV * WIDTH], U8, align_bytes=64)
+        g_row = keep.tile([P, WIDTH], BF16)
+        g_all = keep.tile([P, WIDTH], BF16)
+        ones = keep.tile([P, P], BF16)
+        identity = keep.tile([P, P], F32)
+        one = keep.tile([P, 1], F32)
+        root_of_one = keep.tile([P, 1], F32)
+        q_squares = keep.tile([P, TOKEN_TILES, HEADS], F32)
+        q_dots = keep.tile([P, TOKEN_TILES, HEADS], F32)
+        g_squares = keep.tile([P, HEADS], F32)
+        norms = keep.tile([P, TOKEN_TILES, HEADS], F32)
+        cosines = keep.tile([P, TOKEN_TILES, HEADS], F32)
+        sim_by_token = keep.tile([P, P], F32)
+        sim_by_tile = keep.tile([P, P], F32)
+
+        nc.vector.memset(g_row[:], 0.0)
+        nc.vector.memset(w_planes[:].bitcast(I32), 0)
+        nc.vector.memset(one[:], 1.0)
+        nc.vector.memset(ones[:], 1.0)
+        nc.vector.memset(sim_by_token[:], 0.0)
+        masks.make_identity(nc, identity[:])
+        nc.scalar.dma_start(out=g_row[0:1, :], in_=q_g.rearrange("(o h) d -> o (h d)", o=1))
+        nc.scalar.activation(out=root_of_one[:], in_=one[:], func=ACT.Sqrt)
+
+        def load_x(m):
+            nc.sync.dma_start(out=x_sb[:, m, :], in_=x_tiles[m])
+
+        def load_w(c):
+            cols = slice(2 * WIDTH * c, 2 * WIDTH * (c + 1))
+            nc.sync.dma_start(
+                out=w_sb[:, :, cols].bitcast(I32),
+                in_=w_words[:, :, cols].bitcast(I32).rearrange("g p n -> p g n"),
+            )
+
+        load_x(0)
+        load_x(1)
+        load_w(0)
+        for r in range(4):
+            nc.sync.dma_start(
+                out=w_planes[r:P:32, :, :].bitcast(I32),
+                in_=w_scales[:, r:16:4, :].bitcast(I32).rearrange("g q n -> q g n"),
+            )
+        load_w(1)
+        load_w(2)
+        for m in range(2, TOKEN_TILES):
+            load_x(m)
+
+        def transpose_x(m):
+            words = x_sb[:, m, :].bitcast(F32)
+            halves = side_banks.tile([P, PASSES, 2, P], F32, tag="side")
+            for g in range(PASSES):
+                for u in range(2):
+                    nc.tensor.transpose(
+                        out=halves[:, g, u, :],
+                        in_=words[:, 2 * P * g + u : 2 * P * (g + 1) : 2],
+                        identity=identity[:],
+                    )
+            grouped = regroup.tile([P, K], BF16, align_bytes=64)
+            nc.scalar.copy(
+                out=grouped[:].bitcast(F32).rearrange("p (g r u) -> p g r u", g=PASSES, u=2),
+                in_=halves[:].rearrange("p g u r -> p g r u"),
+            )
+            return grouped
+
+        def quantise_x(m, grouped):
+            nc.vector.quantize_mx(out=x_codes[:, m, :].bitcast(FP8X4), scales=x_scales[:, m, :], in_=grouped[:])
+
+        def project(m, n):
+            product = product_banks.tile([P, BANK], F32)
+            for g in range(PASSES):
+                nc.tensor.matmul_mx(
+                    out=product[:],
+                    lhsT=x_codes[:, m, P * g : P * (g + 1)].bitcast(FP8X4),
+                    lhsT_scale=x_scales[:, m, P * g : P * (g + 1)],
+                    rhs=w_sb[:, g, 2 * BANK * n : 2 * BANK * (n + 1)].bitcast(FP4X4),
+                    rhs_scale=w_planes[:, g, BANK * n : BANK * (n + 1)],
+                    start=(g == 0),
+                    stop=(g == PASSES - 1),
+                )
+            return product
+
+        def sums_of_squares(rows, scale, sums):
+            squares = unread.tile([P, WIDTH], F32)
+            for h in range(HEADS):
+                head = slice(HEAD_DIM * h, HEAD_DIM * (h + 1))
+                nc.scalar.activation(
+                    out=squares[:, head], in_=rows[:, head], func=ACT.Square, scale=scale, accum_out=sums[:, h : h + 1]
+                )
+
+        def dots_with_g(rows, sums):
+            terms = unread.tile([P, WIDTH], F32)
+            for h in range(HEADS):
+                head = slice(HEAD_DIM * h, HEAD_DIM * (h + 1))
+                nc.vector.scalar_tensor_tensor(
+                    out=terms[:, head],
+                    in0=rows[:, head],
+                    scalar=1.0,
+                    in1=g_all[:, head],
+                    op0=ALU.mult,
+                    op1=ALU.mult,
+                    accum_out=sums[:, h : h + 1],
+                )
+
+        quantise_x(0, transpose_x(0))
+        g_spread = side_banks.tile([P, WIDTH], BF16, tag="side")
+        for n in range(BANKS_PER_OUTPUT):
+            cols = slice(BANK * n, BANK * (n + 1))
+            nc.tensor.matmul(out=g_spread[:, cols], lhsT=ones[:], rhs=g_row[:, cols], start=True, stop=True)
+        nc.scalar.copy(out=g_all[:], in_=g_spread[:])
+        sums_of_squares(g_all, float(HEADS), g_squares)
+
+        for m in range(TOKEN_TILES):
+            last = m == TOKEN_TILES - 1
+            if not last:
+                grouped = transpose_x(m + 1)
+
+            q_sb = results.tile([P, WIDTH], F32)
+            for n in range(BANKS_PER_OUTPUT):
+                nc.vector.tensor_copy(out=q_sb[:, BANK * n : BANK * (n + 1)], in_=project(m, n)[:])
+            nc.sync.dma_start(out=q_tiles[m], in_=q_sb[:])
+            if not last:
+                quantise_x(m + 1, grouped)
+            sums_of_squares(q_sb, 1.0, q_squares[:, m, :])
+            dots_with_g(q_sb, q_dots[:, m, :])
+
+            k_sb = results.tile([P, WIDTH], F32)
+            for n in range(BANKS_PER_OUTPUT):
+                nc.scalar.copy(out=k_sb[:, BANK * n : BANK * (n + 1)], in_=project(m, BANKS_PER_OUTPUT + n)[:])
+            nc.sync.dma_start(out=k_tiles[m], in_=k_sb[:])
+
+            if last:
+                nc.vector.tensor_tensor(
+                    out=norms[:],
+                    in0=q_squares[:],
+                    in1=g_squares[:].unsqueeze(1).to_broadcast([P, TOKEN_TILES, HEADS]),
+                    op=ALU.mult,
+                )
+                nc.scalar.activation(out=norms[:], in_=norms[:], func=ACT.Sqrt)
+
+            v_sb = results.tile([P, WIDTH], F32)
+            nc.scalar.copy(out=v_sb[:, 0:BANK], in_=project(m, 2 * BANKS_PER_OUTPUT)[:])
+            nc.vector.tensor_copy(out=v_sb[:, BANK : 2 * BANK], in_=project(m, 2 * BANKS_PER_OUTPUT + 1)[:])
+            nc.sync.dma_start(out=v_tiles[m], in_=v_sb[:])
+
+        nc.vector.reciprocal(out=norms[:], in_=norms[:])
+        nc.vector.tensor_tensor(out=cosines[:], in0=q_dots[:], in1=norms[:], op=ALU.mult)
+        nc.vector.tensor_reduce(out=sim_by_token[:, 0:TOKEN_TILES], in_=cosines[:], axis=AXIS.X, op=ALU.add)
+        sim_rows = side_banks.tile([P, P], F32, tag="side")
+        nc.tensor.transpose(out=sim_rows[:], in_=sim_by_token[:], identity=identity[:])
+        nc.scalar.copy(out=sim_by_tile[0:16, :], in_=sim_rows[0:16, :])
+        first_row = P - REGISTER_TOKENS
+        nc.sync.dma_start(out=sim_out[0:1, 0:first_row], in_=sim_by_tile[0:1, REGISTER_TOKENS:P])
+        nc.sync.dma_start(
+            out=sim_out[0:1, first_row : TOKENS - REGISTER_TOKENS].rearrange("o (m p) -> (o m) p", p=P),
+            in_=sim_by_tile[1:TOKEN_TILES, :],
+        )

@@ -39,11 +39,10 @@ def tile_memeffattention_pa_kernel(tc, x, w_words, w_scales, q_g, q_out, k_out, 
 
     with ExitStack() as ctx:
         keep = ctx.enter_context(tc.tile_pool(name="keep", bufs=1))
-        regroup = ctx.enter_context(tc.tile_pool(name="regroup", bufs=2))
+        regroup = ctx.enter_context(tc.tile_pool(name="regroup", bufs=3))
         results = ctx.enter_context(tc.tile_pool(name="results", bufs=3))
-        unread = ctx.enter_context(tc.tile_pool(name="unread", bufs=2))
-        product_banks = ctx.enter_context(tc.psum_pool(name="product_banks", bufs=6))
-        side_banks = ctx.enter_context(tc.psum_pool(name="side_banks", bufs=2))
+        scratch = ctx.enter_context(tc.tile_pool(name="scratch", bufs=2))
+        banks = ctx.enter_context(tc.psum_pool(name="banks", bufs=8))
         ctx.enter_context(tc.manual_schedule())
 
         x_sb = keep.tile([P, TOKEN_TILES, K], BF16)
@@ -52,7 +51,7 @@ def tile_memeffattention_pa_kernel(tc, x, w_words, w_scales, q_g, q_out, k_out, 
         w_sb = keep.tile([P, PASSES, 2 * QKV * WIDTH], U8, align_bytes=64)
         w_planes = keep.tile([P, PASSES, QKV * WIDTH], U8, align_bytes=64)
         g_row = keep.tile([P, WIDTH], BF16)
-        g_all = keep.tile([P, WIDTH], BF16)
+        g_all = keep.tile([P, WIDTH], F32)
         ones = keep.tile([P, P], BF16)
         identity = keep.tile([P, P], F32)
         one = keep.tile([P, 1], F32)
@@ -65,8 +64,8 @@ def tile_memeffattention_pa_kernel(tc, x, w_words, w_scales, q_g, q_out, k_out, 
         sim_by_token = keep.tile([P, P], F32)
         sim_by_tile = keep.tile([P, P], F32)
 
-        nc.vector.memset(g_row[:], 0.0)
         nc.vector.memset(w_planes[:].bitcast(I32), 0)
+        nc.vector.memset(g_row[:], 0.0)
         nc.vector.memset(one[:], 1.0)
         nc.vector.memset(ones[:], 1.0)
         nc.vector.memset(sim_by_token[:], 0.0)
@@ -74,32 +73,23 @@ def tile_memeffattention_pa_kernel(tc, x, w_words, w_scales, q_g, q_out, k_out, 
         nc.scalar.dma_start(out=g_row[0:1, :], in_=q_g.rearrange("(o h) d -> o (h d)", o=1))
         nc.scalar.activation(out=root_of_one[:], in_=one[:], func=ACT.Sqrt)
 
-        def load_x(m):
+        for m in range(TOKEN_TILES):
             nc.sync.dma_start(out=x_sb[:, m, :], in_=x_tiles[m])
-
-        def load_w(c):
+        for r in range(4):
+            nc.sync.dma_start(
+                out=w_planes[r:P:32, :, :].bitcast(I32),
+                in_=w_scales[:, r:16:4, :].bitcast(I32).rearrange("g q n -> q g n"),
+            )
+        for c in range(QKV):
             cols = slice(2 * WIDTH * c, 2 * WIDTH * (c + 1))
             nc.sync.dma_start(
                 out=w_sb[:, :, cols].bitcast(I32),
                 in_=w_words[:, :, cols].bitcast(I32).rearrange("g p n -> p g n"),
             )
 
-        load_x(0)
-        load_x(1)
-        load_w(0)
-        for r in range(4):
-            nc.sync.dma_start(
-                out=w_planes[r:P:32, :, :].bitcast(I32),
-                in_=w_scales[:, r:16:4, :].bitcast(I32).rearrange("g q n -> q g n"),
-            )
-        load_w(1)
-        load_w(2)
-        for m in range(2, TOKEN_TILES):
-            load_x(m)
-
         def transpose_x(m):
             words = x_sb[:, m, :].bitcast(F32)
-            halves = side_banks.tile([P, PASSES, 2, P], F32, tag="side")
+            halves = banks.tile([P, PASSES, 2, P], F32, tag="bank")
             for g in range(PASSES):
                 for u in range(2):
                     nc.tensor.transpose(
@@ -108,7 +98,8 @@ def tile_memeffattention_pa_kernel(tc, x, w_words, w_scales, q_g, q_out, k_out, 
                         identity=identity[:],
                     )
             grouped = regroup.tile([P, K], BF16, align_bytes=64)
-            nc.scalar.copy(
+            copy_out = nc.scalar.copy if m % 2 == 0 else nc.vector.tensor_copy
+            copy_out(
                 out=grouped[:].bitcast(F32).rearrange("p (g r u) -> p g r u", g=PASSES, u=2),
                 in_=halves[:].rearrange("p g u r -> p g r u"),
             )
@@ -118,7 +109,7 @@ def tile_memeffattention_pa_kernel(tc, x, w_words, w_scales, q_g, q_out, k_out, 
             nc.vector.quantize_mx(out=x_codes[:, m, :].bitcast(FP8X4), scales=x_scales[:, m, :], in_=grouped[:])
 
         def project(m, n):
-            product = product_banks.tile([P, BANK], F32)
+            product = banks.tile([P, BANK], F32, tag="bank")
             for g in range(PASSES):
                 nc.tensor.matmul_mx(
                     out=product[:],
@@ -132,72 +123,80 @@ def tile_memeffattention_pa_kernel(tc, x, w_words, w_scales, q_g, q_out, k_out, 
             return product
 
         def sums_of_squares(rows, scale, sums):
-            squares = unread.tile([P, WIDTH], F32)
+            squares = scratch.tile([P, WIDTH], F32)
             for h in range(HEADS):
                 head = slice(HEAD_DIM * h, HEAD_DIM * (h + 1))
                 nc.scalar.activation(
                     out=squares[:, head], in_=rows[:, head], func=ACT.Square, scale=scale, accum_out=sums[:, h : h + 1]
                 )
 
-        def dots_with_g(rows, sums):
-            terms = unread.tile([P, WIDTH], F32)
-            for h in range(HEADS):
-                head = slice(HEAD_DIM * h, HEAD_DIM * (h + 1))
-                nc.vector.scalar_tensor_tensor(
-                    out=terms[:, head],
-                    in0=rows[:, head],
-                    scalar=1.0,
-                    in1=g_all[:, head],
-                    op0=ALU.mult,
-                    op1=ALU.mult,
-                    accum_out=sums[:, h : h + 1],
-                )
+        def q_part(m):
+            q_sb = results.tile([P, WIDTH], F32)
+            terms = scratch.tile([P, WIDTH], F32)
+            for n in range(BANKS_PER_OUTPUT):
+                cols = slice(BANK * n, BANK * (n + 1))
+                nc.vector.tensor_copy(out=q_sb[:, cols], in_=project(m, n)[:])
+                nc.gpsimd.tensor_tensor(out=terms[:, cols], in0=q_sb[:, cols], in1=g_all[:, cols], op=ALU.mult)
+            nc.sync.dma_start(out=q_tiles[m], in_=q_sb[:])
+            sums_of_squares(q_sb, 1.0, q_squares[:, m, :])
+            return terms
 
-        quantise_x(0, transpose_x(0))
-        g_spread = side_banks.tile([P, WIDTH], BF16, tag="side")
+        def dots_with_g(m, terms):
+            nc.vector.tensor_reduce(
+                out=q_dots[:, m, :], in_=terms[:].rearrange("p (h d) -> p h d", h=HEADS), axis=AXIS.X, op=ALU.add
+            )
+
+        def k_part(m):
+            k_sb = results.tile([P, WIDTH], F32)
+            for n in range(BANKS_PER_OUTPUT):
+                nc.scalar.copy(out=k_sb[:, BANK * n : BANK * (n + 1)], in_=project(m, BANKS_PER_OUTPUT + n)[:])
+            nc.sync.dma_start(out=k_tiles[m], in_=k_sb[:])
+
+        def v_part(m):
+            v_sb = results.tile([P, WIDTH], F32)
+            nc.scalar.copy(out=v_sb[:, 0:BANK], in_=project(m, 2 * BANKS_PER_OUTPUT)[:])
+            nc.vector.tensor_copy(out=v_sb[:, BANK : 2 * BANK], in_=project(m, 2 * BANKS_PER_OUTPUT + 1)[:])
+            nc.sync.dma_start(out=v_tiles[m], in_=v_sb[:])
+
+        grouped = [transpose_x(0)]
+        for m in range(1, TOKEN_TILES):
+            grouped.append(transpose_x(m))
+            quantise_x(m - 1, grouped[m - 1])
+        quantise_x(TOKEN_TILES - 1, grouped[TOKEN_TILES - 1])
+
+        g_spread = banks.tile([P, WIDTH], BF16, tag="bank")
         for n in range(BANKS_PER_OUTPUT):
             cols = slice(BANK * n, BANK * (n + 1))
             nc.tensor.matmul(out=g_spread[:, cols], lhsT=ones[:], rhs=g_row[:, cols], start=True, stop=True)
         nc.scalar.copy(out=g_all[:], in_=g_spread[:])
         sums_of_squares(g_all, float(HEADS), g_squares)
 
+        terms_of_tile = []
         for m in range(TOKEN_TILES):
-            last = m == TOKEN_TILES - 1
-            if not last:
-                grouped = transpose_x(m + 1)
+            terms_of_tile.append(q_part(m))
+            if m >= 1:
+                dots_with_g(m - 1, terms_of_tile[m - 1])
+            if m >= 2:
+                k_part(m - 2)
+                v_part(m - 2)
 
-            q_sb = results.tile([P, WIDTH], F32)
-            for n in range(BANKS_PER_OUTPUT):
-                nc.vector.tensor_copy(out=q_sb[:, BANK * n : BANK * (n + 1)], in_=project(m, n)[:])
-            nc.sync.dma_start(out=q_tiles[m], in_=q_sb[:])
-            if not last:
-                quantise_x(m + 1, grouped)
-            sums_of_squares(q_sb, 1.0, q_squares[:, m, :])
-            dots_with_g(q_sb, q_dots[:, m, :])
-
-            k_sb = results.tile([P, WIDTH], F32)
-            for n in range(BANKS_PER_OUTPUT):
-                nc.scalar.copy(out=k_sb[:, BANK * n : BANK * (n + 1)], in_=project(m, BANKS_PER_OUTPUT + n)[:])
-            nc.sync.dma_start(out=k_tiles[m], in_=k_sb[:])
-
-            if last:
-                nc.vector.tensor_tensor(
-                    out=norms[:],
-                    in0=q_squares[:],
-                    in1=g_squares[:].unsqueeze(1).to_broadcast([P, TOKEN_TILES, HEADS]),
-                    op=ALU.mult,
-                )
-                nc.scalar.activation(out=norms[:], in_=norms[:], func=ACT.Sqrt)
-
-            v_sb = results.tile([P, WIDTH], F32)
-            nc.scalar.copy(out=v_sb[:, 0:BANK], in_=project(m, 2 * BANKS_PER_OUTPUT)[:])
-            nc.vector.tensor_copy(out=v_sb[:, BANK : 2 * BANK], in_=project(m, 2 * BANKS_PER_OUTPUT + 1)[:])
-            nc.sync.dma_start(out=v_tiles[m], in_=v_sb[:])
-
+        last = TOKEN_TILES - 1
+        dots_with_g(last, terms_of_tile[last])
+        nc.vector.tensor_tensor(
+            out=norms[:],
+            in0=q_squares[:],
+            in1=g_squares[:].unsqueeze(1).to_broadcast([P, TOKEN_TILES, HEADS]),
+            op=ALU.mult,
+        )
+        k_part(last - 1)
+        nc.scalar.activation(out=norms[:], in_=norms[:], func=ACT.Sqrt)
         nc.vector.reciprocal(out=norms[:], in_=norms[:])
+        v_part(last - 1)
         nc.vector.tensor_tensor(out=cosines[:], in0=q_dots[:], in1=norms[:], op=ALU.mult)
         nc.vector.tensor_reduce(out=sim_by_token[:, 0:TOKEN_TILES], in_=cosines[:], axis=AXIS.X, op=ALU.add)
-        sim_rows = side_banks.tile([P, P], F32, tag="side")
+        k_part(last)
+        v_part(last)
+        sim_rows = banks.tile([P, P], F32, tag="bank")
         nc.tensor.transpose(out=sim_rows[:], in_=sim_by_token[:], identity=identity[:])
         nc.scalar.copy(out=sim_by_tile[0:16, :], in_=sim_rows[0:16, :])
         first_row = P - REGISTER_TOKENS

@@ -26,13 +26,14 @@ PASSES = K // (4 * P)
 BANK = 512
 BANKS_PER_OUTPUT = WIDTH // BANK
 QKV = 3
+STATISTICS = 6
 
 FLOPS = 2 * TOKENS * K * QKV * WIDTH
 
 
 def tile_memeffattention_pa_kernel(tc, x, w_words, w_scales, q_g, q_out, k_out, v_out, sim_out):
     nc = tc.nc
-    x_tiles = x.rearrange("b (m p) k -> (b m) p k", p=P)
+    x_pairs = x.rearrange("b (j i p) k -> (b j) p i k", i=2, p=P)
     q_tiles = q_out.rearrange("b (m p) h d -> (b m) p (h d)", p=P)
     k_tiles = k_out.rearrange("b (m p) h d -> (b m) p (h d)", p=P)
     v_tiles = v_out.rearrange("b (m p) h d -> (b m) p (h d)", p=P)
@@ -41,14 +42,14 @@ def tile_memeffattention_pa_kernel(tc, x, w_words, w_scales, q_g, q_out, k_out, 
         keep = ctx.enter_context(tc.tile_pool(name="keep", bufs=1))
         regroup = ctx.enter_context(tc.tile_pool(name="regroup", bufs=3))
         results = ctx.enter_context(tc.tile_pool(name="results", bufs=3))
-        scratch = ctx.enter_context(tc.tile_pool(name="scratch", bufs=2))
+        scratch = ctx.enter_context(tc.tile_pool(name="scratch", bufs=3))
         banks = ctx.enter_context(tc.psum_pool(name="banks", bufs=8))
         ctx.enter_context(tc.manual_schedule())
 
         x_sb = keep.tile([P, TOKEN_TILES, K], BF16)
         x_codes = keep.tile([P, TOKEN_TILES, PASSES * P], U32, align_bytes=64)
         x_scales = keep.tile([P, TOKEN_TILES, PASSES * P], U8, align_bytes=64)
-        w_sb = keep.tile([P, PASSES, 2 * QKV * WIDTH], U8, align_bytes=64)
+        w_sb = keep.tile([P, QKV, PASSES, 2 * WIDTH], U8, align_bytes=64)
         w_planes = keep.tile([P, PASSES, QKV * WIDTH], U8, align_bytes=64)
         g_row = keep.tile([P, WIDTH], BF16)
         g_all = keep.tile([P, WIDTH], F32)
@@ -56,9 +57,10 @@ def tile_memeffattention_pa_kernel(tc, x, w_words, w_scales, q_g, q_out, k_out, 
         identity = keep.tile([P, P], F32)
         one = keep.tile([P, 1], F32)
         root_of_one = keep.tile([P, 1], F32)
-        q_squares = keep.tile([P, TOKEN_TILES, HEADS], F32)
+        statistics = keep.tile([P, TOKEN_TILES + 1, HEADS, STATISTICS], F32)
+        half_sums = keep.tile([P, TOKEN_TILES + 1, HEADS, 2], F32)
+        squares = keep.tile([P, TOKEN_TILES + 1, HEADS], F32)
         q_dots = keep.tile([P, TOKEN_TILES, HEADS], F32)
-        g_squares = keep.tile([P, HEADS], F32)
         norms = keep.tile([P, TOKEN_TILES, HEADS], F32)
         cosines = keep.tile([P, TOKEN_TILES, HEADS], F32)
         sim_by_token = keep.tile([P, P], F32)
@@ -70,11 +72,11 @@ def tile_memeffattention_pa_kernel(tc, x, w_words, w_scales, q_g, q_out, k_out, 
         nc.vector.memset(ones[:], 1.0)
         nc.vector.memset(sim_by_token[:], 0.0)
         masks.make_identity(nc, identity[:])
-        nc.scalar.dma_start(out=g_row[0:1, :], in_=q_g.rearrange("(o h) d -> o (h d)", o=1))
         nc.scalar.activation(out=root_of_one[:], in_=one[:], func=ACT.Sqrt)
 
-        for m in range(TOKEN_TILES):
-            nc.sync.dma_start(out=x_sb[:, m, :], in_=x_tiles[m])
+        for j in range(TOKEN_TILES // 2):
+            nc.sync.dma_start(out=x_sb[:, 2 * j : 2 * j + 2, :], in_=x_pairs[j])
+        nc.sync.dma_start(out=g_row[0:1, :], in_=q_g.rearrange("(o h) d -> o (h d)", o=1))
         for r in range(4):
             nc.sync.dma_start(
                 out=w_planes[r:P:32, :, :].bitcast(I32),
@@ -83,7 +85,7 @@ def tile_memeffattention_pa_kernel(tc, x, w_words, w_scales, q_g, q_out, k_out, 
         for c in range(QKV):
             cols = slice(2 * WIDTH * c, 2 * WIDTH * (c + 1))
             nc.sync.dma_start(
-                out=w_sb[:, :, cols].bitcast(I32),
+                out=w_sb[:, c, :, :].bitcast(I32),
                 in_=w_words[:, :, cols].bitcast(I32).rearrange("g p n -> p g n"),
             )
 
@@ -108,37 +110,34 @@ def tile_memeffattention_pa_kernel(tc, x, w_words, w_scales, q_g, q_out, k_out, 
         def quantise_x(m, grouped):
             nc.vector.quantize_mx(out=x_codes[:, m, :].bitcast(FP8X4), scales=x_scales[:, m, :], in_=grouped[:])
 
-        def project(m, n):
+        def project(m, c, n):
             product = banks.tile([P, BANK], F32, tag="bank")
+            plane_cols = slice(WIDTH * c + BANK * n, WIDTH * c + BANK * (n + 1))
             for g in range(PASSES):
                 nc.tensor.matmul_mx(
                     out=product[:],
                     lhsT=x_codes[:, m, P * g : P * (g + 1)].bitcast(FP8X4),
                     lhsT_scale=x_scales[:, m, P * g : P * (g + 1)],
-                    rhs=w_sb[:, g, 2 * BANK * n : 2 * BANK * (n + 1)].bitcast(FP4X4),
-                    rhs_scale=w_planes[:, g, BANK * n : BANK * (n + 1)],
+                    rhs=w_sb[:, c, g, 2 * BANK * n : 2 * BANK * (n + 1)].bitcast(FP4X4),
+                    rhs_scale=w_planes[:, g, plane_cols],
                     start=(g == 0),
                     stop=(g == PASSES - 1),
                 )
             return product
 
-        def sums_of_squares(rows, scale, sums):
-            squares = scratch.tile([P, WIDTH], F32)
+        def head_statistics(rows, row):
             for h in range(HEADS):
-                head = slice(HEAD_DIM * h, HEAD_DIM * (h + 1))
-                nc.scalar.activation(
-                    out=squares[:, head], in_=rows[:, head], func=ACT.Square, scale=scale, accum_out=sums[:, h : h + 1]
-                )
+                nc.vector.bn_stats(out=statistics[:, row, h, :], in_=rows[:, HEAD_DIM * h : HEAD_DIM * (h + 1)])
 
         def q_part(m):
             q_sb = results.tile([P, WIDTH], F32)
             terms = scratch.tile([P, WIDTH], F32)
             for n in range(BANKS_PER_OUTPUT):
                 cols = slice(BANK * n, BANK * (n + 1))
-                nc.vector.tensor_copy(out=q_sb[:, cols], in_=project(m, n)[:])
+                nc.scalar.copy(out=q_sb[:, cols], in_=project(m, 0, n)[:])
                 nc.gpsimd.tensor_tensor(out=terms[:, cols], in0=q_sb[:, cols], in1=g_all[:, cols], op=ALU.mult)
             nc.sync.dma_start(out=q_tiles[m], in_=q_sb[:])
-            sums_of_squares(q_sb, 1.0, q_squares[:, m, :])
+            head_statistics(q_sb, m)
             return terms
 
         def dots_with_g(m, terms):
@@ -149,13 +148,13 @@ def tile_memeffattention_pa_kernel(tc, x, w_words, w_scales, q_g, q_out, k_out, 
         def k_part(m):
             k_sb = results.tile([P, WIDTH], F32)
             for n in range(BANKS_PER_OUTPUT):
-                nc.scalar.copy(out=k_sb[:, BANK * n : BANK * (n + 1)], in_=project(m, BANKS_PER_OUTPUT + n)[:])
+                nc.scalar.copy(out=k_sb[:, BANK * n : BANK * (n + 1)], in_=project(m, 1, n)[:])
             nc.sync.dma_start(out=k_tiles[m], in_=k_sb[:])
 
         def v_part(m):
             v_sb = results.tile([P, WIDTH], F32)
-            nc.scalar.copy(out=v_sb[:, 0:BANK], in_=project(m, 2 * BANKS_PER_OUTPUT)[:])
-            nc.vector.tensor_copy(out=v_sb[:, BANK : 2 * BANK], in_=project(m, 2 * BANKS_PER_OUTPUT + 1)[:])
+            nc.scalar.copy(out=v_sb[:, 0:BANK], in_=project(m, 2, 0)[:])
+            nc.vector.tensor_copy(out=v_sb[:, BANK : 2 * BANK], in_=project(m, 2, 1)[:])
             nc.sync.dma_start(out=v_tiles[m], in_=v_sb[:])
 
         grouped = [transpose_x(0)]
@@ -169,7 +168,7 @@ def tile_memeffattention_pa_kernel(tc, x, w_words, w_scales, q_g, q_out, k_out, 
             cols = slice(BANK * n, BANK * (n + 1))
             nc.tensor.matmul(out=g_spread[:, cols], lhsT=ones[:], rhs=g_row[:, cols], start=True, stop=True)
         nc.scalar.copy(out=g_all[:], in_=g_spread[:])
-        sums_of_squares(g_all, float(HEADS), g_squares)
+        head_statistics(g_all, TOKEN_TILES)
 
         terms_of_tile = []
         for m in range(TOKEN_TILES):
@@ -182,14 +181,21 @@ def tile_memeffattention_pa_kernel(tc, x, w_words, w_scales, q_g, q_out, k_out, 
 
         last = TOKEN_TILES - 1
         dots_with_g(last, terms_of_tile[last])
+        means = statistics[:, :, :, 1:STATISTICS:3]
+        spreads = statistics[:, :, :, 2:STATISTICS:3]
+        nc.vector.tensor_tensor(out=half_sums[:], in0=means, in1=means, op=ALU.mult)
+        nc.vector.scalar_tensor_tensor(
+            out=half_sums[:], in0=half_sums[:], scalar=float(HEAD_DIM // 2), in1=spreads, op0=ALU.mult, op1=ALU.add
+        )
+        nc.vector.tensor_reduce(out=squares[:], in_=half_sums[:], axis=AXIS.X, op=ALU.add)
         nc.vector.tensor_tensor(
             out=norms[:],
-            in0=q_squares[:],
-            in1=g_squares[:].unsqueeze(1).to_broadcast([P, TOKEN_TILES, HEADS]),
+            in0=squares[:, 0:TOKEN_TILES, :],
+            in1=squares[:, TOKEN_TILES : TOKEN_TILES + 1, :].to_broadcast([P, TOKEN_TILES, HEADS]),
             op=ALU.mult,
         )
         k_part(last - 1)
-        nc.scalar.activation(out=norms[:], in_=norms[:], func=ACT.Sqrt)
+        nc.scalar.activation(out=norms[:], in_=norms[:], func=ACT.Sqrt, scale=float(HEADS * HEADS))
         nc.vector.reciprocal(out=norms[:], in_=norms[:])
         v_part(last - 1)
         nc.vector.tensor_tensor(out=cosines[:], in0=q_dots[:], in1=norms[:], op=ALU.mult)

@@ -50,7 +50,7 @@ def tile_memeffattention_pa_kernel(tc, x, w_words, w_scales, q_g, q_out, k_out, 
         x_codes = keep.tile([P, TOKEN_TILES, PASSES * P], U32, align_bytes=64)
         x_scales = keep.tile([P, TOKEN_TILES, PASSES * P], U8, align_bytes=64)
         w_sb = keep.tile([P, QKV, PASSES, 2 * WIDTH], U8, align_bytes=64)
-        w_planes = keep.tile([P, PASSES, QKV * WIDTH], U8, align_bytes=64)
+        w_planes = keep.tile([P, QKV, PASSES, WIDTH], U8, align_bytes=64)
         g_row = keep.tile([P, WIDTH], BF16)
         g_all = keep.tile([P, WIDTH], F32)
         ones = keep.tile([P, P], BF16)
@@ -77,16 +77,15 @@ def tile_memeffattention_pa_kernel(tc, x, w_words, w_scales, q_g, q_out, k_out, 
         for j in range(TOKEN_TILES // 2):
             nc.sync.dma_start(out=x_sb[:, 2 * j : 2 * j + 2, :], in_=x_pairs[j])
         nc.sync.dma_start(out=g_row[0:1, :], in_=q_g.rearrange("(o h) d -> o (h d)", o=1))
-        for r in range(4):
-            nc.sync.dma_start(
-                out=w_planes[r:P:32, :, :].bitcast(I32),
-                in_=w_scales[:, r:16:4, :].bitcast(I32).rearrange("g q n -> q g n"),
-            )
         for c in range(QKV):
-            cols = slice(2 * WIDTH * c, 2 * WIDTH * (c + 1))
+            for r in range(4):
+                nc.sync.dma_start(
+                    out=w_planes[r:P:32, c, :, :].bitcast(I32),
+                    in_=w_scales[:, r:16:4, WIDTH * c : WIDTH * (c + 1)].bitcast(I32).rearrange("g q n -> q g n"),
+                )
             nc.sync.dma_start(
                 out=w_sb[:, c, :, :].bitcast(I32),
-                in_=w_words[:, :, cols].bitcast(I32).rearrange("g p n -> p g n"),
+                in_=w_words[:, :, 2 * WIDTH * c : 2 * WIDTH * (c + 1)].bitcast(I32).rearrange("g p n -> p g n"),
             )
 
         def transpose_x(m):
@@ -112,14 +111,13 @@ def tile_memeffattention_pa_kernel(tc, x, w_words, w_scales, q_g, q_out, k_out, 
 
         def project(m, c, n):
             product = banks.tile([P, BANK], F32, tag="bank")
-            plane_cols = slice(WIDTH * c + BANK * n, WIDTH * c + BANK * (n + 1))
             for g in range(PASSES):
                 nc.tensor.matmul_mx(
                     out=product[:],
                     lhsT=x_codes[:, m, P * g : P * (g + 1)].bitcast(FP8X4),
                     lhsT_scale=x_scales[:, m, P * g : P * (g + 1)],
                     rhs=w_sb[:, c, g, 2 * BANK * n : 2 * BANK * (n + 1)].bitcast(FP4X4),
-                    rhs_scale=w_planes[:, g, plane_cols],
+                    rhs_scale=w_planes[:, c, g, BANK * n : BANK * (n + 1)],
                     start=(g == 0),
                     stop=(g == PASSES - 1),
                 )
@@ -173,11 +171,11 @@ def tile_memeffattention_pa_kernel(tc, x, w_words, w_scales, q_g, q_out, k_out, 
         terms_of_tile = []
         for m in range(TOKEN_TILES):
             terms_of_tile.append(q_part(m))
-            if m >= 1:
-                dots_with_g(m - 1, terms_of_tile[m - 1])
             if m >= 2:
                 k_part(m - 2)
                 v_part(m - 2)
+            if m >= 1:
+                dots_with_g(m - 1, terms_of_tile[m - 1])
 
         last = TOKEN_TILES - 1
         dots_with_g(last, terms_of_tile[last])

@@ -50,7 +50,7 @@ def tile_memeffattention_pa_kernel(tc, x, w_words, w_scales, q_g, q_out, k_out, 
         x_codes = keep.tile([P, TOKEN_TILES, PASSES * P], U32, align_bytes=64)
         x_scales = keep.tile([P, TOKEN_TILES, PASSES * P], U8, align_bytes=64)
         w_sb = keep.tile([P, QKV, PASSES, 2 * WIDTH], U8, align_bytes=64)
-        w_planes = keep.tile([P, QKV, PASSES, WIDTH], U8, align_bytes=64)
+        w_planes = keep.tile([P, PASSES, QKV * WIDTH], U8, align_bytes=64)
         g_row = keep.tile([P, WIDTH], BF16)
         g_all = keep.tile([P, WIDTH], F32)
         ones = keep.tile([P, P], BF16)
@@ -77,15 +77,16 @@ def tile_memeffattention_pa_kernel(tc, x, w_words, w_scales, q_g, q_out, k_out, 
         for j in range(TOKEN_TILES // 2):
             nc.sync.dma_start(out=x_sb[:, 2 * j : 2 * j + 2, :], in_=x_pairs[j])
         nc.sync.dma_start(out=g_row[0:1, :], in_=q_g.rearrange("(o h) d -> o (h d)", o=1))
+        for r in range(4):
+            nc.sync.dma_start(
+                out=w_planes[r:P:32, :, :].bitcast(I32),
+                in_=w_scales[:, r:16:4, :].bitcast(I32).rearrange("g q n -> q g n"),
+            )
         for c in range(QKV):
-            for r in range(4):
-                nc.sync.dma_start(
-                    out=w_planes[r:P:32, c, :, :].bitcast(I32),
-                    in_=w_scales[:, r:16:4, WIDTH * c : WIDTH * (c + 1)].bitcast(I32).rearrange("g q n -> q g n"),
-                )
+            cols = slice(2 * WIDTH * c, 2 * WIDTH * (c + 1))
             nc.sync.dma_start(
                 out=w_sb[:, c, :, :].bitcast(I32),
-                in_=w_words[:, :, 2 * WIDTH * c : 2 * WIDTH * (c + 1)].bitcast(I32).rearrange("g p n -> p g n"),
+                in_=w_words[:, :, cols].bitcast(I32).rearrange("g p n -> p g n"),
             )
 
         def transpose_x(m):
@@ -111,13 +112,14 @@ def tile_memeffattention_pa_kernel(tc, x, w_words, w_scales, q_g, q_out, k_out, 
 
         def project(m, c, n):
             product = banks.tile([P, BANK], F32, tag="bank")
+            plane_cols = slice(WIDTH * c + BANK * n, WIDTH * c + BANK * (n + 1))
             for g in range(PASSES):
                 nc.tensor.matmul_mx(
                     out=product[:],
                     lhsT=x_codes[:, m, P * g : P * (g + 1)].bitcast(FP8X4),
                     lhsT_scale=x_scales[:, m, P * g : P * (g + 1)],
                     rhs=w_sb[:, c, g, 2 * BANK * n : 2 * BANK * (n + 1)].bitcast(FP4X4),
-                    rhs_scale=w_planes[:, c, g, BANK * n : BANK * (n + 1)],
+                    rhs_scale=w_planes[:, g, plane_cols],
                     start=(g == 0),
                     stop=(g == PASSES - 1),
                 )
@@ -151,9 +153,14 @@ def tile_memeffattention_pa_kernel(tc, x, w_words, w_scales, q_g, q_out, k_out, 
 
         def v_part(m):
             v_sb = results.tile([P, WIDTH], F32)
-            nc.scalar.copy(out=v_sb[:, 0:BANK], in_=project(m, 2, 0)[:])
-            nc.vector.tensor_copy(out=v_sb[:, BANK : 2 * BANK], in_=project(m, 2, 1)[:])
-            nc.sync.dma_start(out=v_tiles[m], in_=v_sb[:])
+            at_the_end = m == TOKEN_TILES - 1
+            for n in range(BANKS_PER_OUTPUT):
+                cols = slice(BANK * n, BANK * (n + 1))
+                nc.scalar.copy(out=v_sb[:, cols], in_=project(m, 2, n)[:])
+                if at_the_end:
+                    nc.sync.dma_start(out=v_tiles[m][:, cols], in_=v_sb[:, cols])
+            if not at_the_end:
+                nc.sync.dma_start(out=v_tiles[m], in_=v_sb[:])
 
         grouped = [transpose_x(0)]
         for m in range(1, TOKEN_TILES):
@@ -165,17 +172,17 @@ def tile_memeffattention_pa_kernel(tc, x, w_words, w_scales, q_g, q_out, k_out, 
         for n in range(BANKS_PER_OUTPUT):
             cols = slice(BANK * n, BANK * (n + 1))
             nc.tensor.matmul(out=g_spread[:, cols], lhsT=ones[:], rhs=g_row[:, cols], start=True, stop=True)
-        nc.scalar.copy(out=g_all[:], in_=g_spread[:])
+        nc.vector.tensor_copy(out=g_all[:], in_=g_spread[:])
         head_statistics(g_all, TOKEN_TILES)
 
         terms_of_tile = []
         for m in range(TOKEN_TILES):
             terms_of_tile.append(q_part(m))
+            if m >= 1:
+                dots_with_g(m - 1, terms_of_tile[m - 1])
             if m >= 2:
                 k_part(m - 2)
                 v_part(m - 2)
-            if m >= 1:
-                dots_with_g(m - 1, terms_of_tile[m - 1])
 
         last = TOKEN_TILES - 1
         dots_with_g(last, terms_of_tile[last])
@@ -193,9 +200,9 @@ def tile_memeffattention_pa_kernel(tc, x, w_words, w_scales, q_g, q_out, k_out, 
             op=ALU.mult,
         )
         k_part(last - 1)
+        v_part(last - 1)
         nc.scalar.activation(out=norms[:], in_=norms[:], func=ACT.Sqrt, scale=float(HEADS * HEADS))
         nc.vector.reciprocal(out=norms[:], in_=norms[:])
-        v_part(last - 1)
         nc.vector.tensor_tensor(out=cosines[:], in0=q_dots[:], in1=norms[:], op=ALU.mult)
         nc.vector.tensor_reduce(out=sim_by_token[:, 0:TOKEN_TILES], in_=cosines[:], axis=AXIS.X, op=ALU.add)
         k_part(last)

@@ -57,8 +57,7 @@ def tile_memeffattention_pa_kernel(tc, x, w_words, w_scales, q_g, q_out, k_out, 
         identity = keep.tile([P, P], F32)
         one = keep.tile([P, 1], F32)
         root_of_one = keep.tile([P, 1], F32)
-        statistics = keep.tile([P, TOKEN_TILES + 1, HEADS, STATISTICS], F32)
-        half_sums = keep.tile([P, TOKEN_TILES + 1, HEADS, 2], F32)
+        statistics = keep.tile([P, TOKEN_TILES + 1, HEADS // 2, STATISTICS], F32)
         squares = keep.tile([P, TOKEN_TILES + 1, HEADS], F32)
         q_dots = keep.tile([P, TOKEN_TILES, HEADS], F32)
         norms = keep.tile([P, TOKEN_TILES, HEADS], F32)
@@ -126,8 +125,11 @@ def tile_memeffattention_pa_kernel(tc, x, w_words, w_scales, q_g, q_out, k_out, 
             return product
 
         def head_statistics(rows, row):
-            for h in range(HEADS):
-                nc.vector.bn_stats(out=statistics[:, row, h, :], in_=rows[:, HEAD_DIM * h : HEAD_DIM * (h + 1)])
+            for pair in range(HEADS // 2):
+                nc.vector.bn_stats(
+                    out=statistics[:, row, pair, :],
+                    in_=rows[:, 2 * HEAD_DIM * pair : 2 * HEAD_DIM * (pair + 1)].rearrange("p (s d) -> p d s", s=2),
+                )
 
         def q_part(m):
             q_sb = results.tile([P, WIDTH], F32)
@@ -186,13 +188,13 @@ def tile_memeffattention_pa_kernel(tc, x, w_words, w_scales, q_g, q_out, k_out, 
 
         last = TOKEN_TILES - 1
         dots_with_g(last, terms_of_tile[last])
-        means = statistics[:, :, :, 1:STATISTICS:3]
-        spreads = statistics[:, :, :, 2:STATISTICS:3]
-        nc.vector.tensor_tensor(out=half_sums[:], in0=means, in1=means, op=ALU.mult)
+        by_head = statistics[:].rearrange("p m c (s t) -> p m (c s) t", s=2)
+        means = by_head[:, :, :, 1]
+        spreads = by_head[:, :, :, 2]
+        nc.vector.tensor_tensor(out=squares[:], in0=means, in1=means, op=ALU.mult)
         nc.vector.scalar_tensor_tensor(
-            out=half_sums[:], in0=half_sums[:], scalar=float(HEAD_DIM // 2), in1=spreads, op0=ALU.mult, op1=ALU.add
+            out=squares[:], in0=squares[:], scalar=float(HEAD_DIM), in1=spreads, op0=ALU.mult, op1=ALU.add
         )
-        nc.vector.tensor_reduce(out=squares[:], in_=half_sums[:], axis=AXIS.X, op=ALU.add)
         nc.vector.tensor_tensor(
             out=norms[:],
             in0=squares[:, 0:TOKEN_TILES, :],

@@ -27,6 +27,7 @@ BANK = 512
 BANKS_PER_OUTPUT = WIDTH // BANK
 QKV = 3
 STATISTICS = 6
+WARM_UP = 5
 
 FLOPS = 2 * TOKENS * K * QKV * WIDTH
 
@@ -54,6 +55,7 @@ def tile_memeffattention_pa_kernel(tc, x, w_words, w_scales, q_g, q_out, k_out, 
         g_row = keep.tile([P, WIDTH], BF16)
         g_all = keep.tile([P, WIDTH], F32)
         ones = keep.tile([P, P], BF16)
+        idle_rows = keep.tile([P, BANK], BF16)
         identity = keep.tile([P, P], F32)
         one = keep.tile([P, 1], F32)
         root_of_one = keep.tile([P, 1], F32)
@@ -65,10 +67,11 @@ def tile_memeffattention_pa_kernel(tc, x, w_words, w_scales, q_g, q_out, k_out, 
         sim_by_token = keep.tile([P, P], F32)
         sim_by_tile = keep.tile([P, P], F32)
 
+        nc.vector.memset(ones[:], 1.0)
+        nc.vector.memset(idle_rows[:], 0.0)
         nc.vector.memset(w_planes[:].bitcast(I32), 0)
         nc.vector.memset(g_row[:], 0.0)
         nc.vector.memset(one[:], 1.0)
-        nc.vector.memset(ones[:], 1.0)
         nc.vector.memset(sim_by_token[:], 0.0)
         masks.make_identity(nc, identity[:])
         nc.scalar.activation(out=root_of_one[:], in_=one[:], func=ACT.Sqrt)
@@ -164,9 +167,18 @@ def tile_memeffattention_pa_kernel(tc, x, w_words, w_scales, q_g, q_out, k_out, 
             if not at_the_end:
                 nc.sync.dma_start(out=v_tiles[m], in_=v_sb[:])
 
+        idle_product = banks.tile([P, BANK], F32, tag="bank")
+
+        def keep_the_clock_up(count):
+            for repeat in range(count):
+                nc.tensor.matmul(out=idle_product[:], lhsT=ones[:], rhs=idle_rows[:], start=True, stop=True)
+
+        keep_the_clock_up(WARM_UP)
         grouped = [transpose_x(0)]
+        keep_the_clock_up(1)
         for m in range(1, TOKEN_TILES):
             grouped.append(transpose_x(m))
+            keep_the_clock_up(1)
             quantise_x(m - 1, grouped[m - 1])
         quantise_x(TOKEN_TILES - 1, grouped[TOKEN_TILES - 1])
 

@@ -21,77 +21,102 @@ HEADS = 8
 HEAD_DIM = 128
 WIDTH = HEADS * HEAD_DIM
 REGISTER_TOKENS = 5
-TOKEN_TILES = TOKENS // P
+TILES = TOKENS // P
+PAIRS = TILES // 2
 PASSES = K // (4 * P)
 BANK = 512
-BANKS_PER_OUTPUT = WIDTH // BANK
-QKV = 3
+HALVES = WIDTH // BANK
 STATISTICS = 6
-WARM_UP = 5
+WARM_UP = 4
 
-FLOPS = 2 * TOKENS * K * QKV * WIDTH
+FLOPS = 2 * TOKENS * K * 3 * WIDTH
 
 
 def tile_memeffattention_pa_kernel(tc, x, w_words, w_scales, q_g, q_out, k_out, v_out, sim_out):
     nc = tc.nc
-    x_pairs = x.rearrange("b (j i p) k -> (b j) p i k", i=2, p=P)
-    q_tiles = q_out.rearrange("b (m p) h d -> (b m) p (h d)", p=P)
-    k_tiles = k_out.rearrange("b (m p) h d -> (b m) p (h d)", p=P)
-    v_tiles = v_out.rearrange("b (m p) h d -> (b m) p (h d)", p=P)
+    x_pairs = x.rearrange("b (j p i) k -> p (b j) (i k)", p=P, i=2)
+    q_pairs = q_out.rearrange("b (j p i) h d -> (b j) p i (h d)", p=P, i=2)
+    k_pairs = k_out.rearrange("b (j p i) h d -> (b j) p i (h d)", p=P, i=2)
+    v_pairs = v_out.rearrange("b (j p i) h d -> (b j) p i (h d)", p=P, i=2)
 
     with ExitStack() as ctx:
         keep = ctx.enter_context(tc.tile_pool(name="keep", bufs=1))
-        regroup = ctx.enter_context(tc.tile_pool(name="regroup", bufs=3))
-        results = ctx.enter_context(tc.tile_pool(name="results", bufs=3))
-        scratch = ctx.enter_context(tc.tile_pool(name="scratch", bufs=3))
+        regroup = ctx.enter_context(tc.tile_pool(name="regroup", bufs=4))
+        results = ctx.enter_context(tc.tile_pool(name="results", bufs=12))
+        scratch = ctx.enter_context(tc.tile_pool(name="scratch", bufs=4))
         banks = ctx.enter_context(tc.psum_pool(name="banks", bufs=8))
         ctx.enter_context(tc.manual_schedule())
 
-        x_sb = keep.tile([P, TOKEN_TILES, K], BF16)
-        x_codes = keep.tile([P, TOKEN_TILES, PASSES * P], U32, align_bytes=64)
-        x_scales = keep.tile([P, TOKEN_TILES, PASSES * P], U8, align_bytes=64)
-        w_sb = keep.tile([P, QKV, PASSES, 2 * WIDTH], U8, align_bytes=64)
-        w_planes = keep.tile([P, PASSES, QKV * WIDTH], U8, align_bytes=64)
+        x_sb = keep.tile([P, TILES, K], BF16)
+        x_codes = keep.tile([P, TILES, PASSES * P], U32, align_bytes=64)
+        x_scales = keep.tile([P, TILES, PASSES * P], U8, align_bytes=64)
+        q_words = keep.tile([P, PASSES, 2 * WIDTH], U8, align_bytes=64)
+        kv_words = keep.tile([P, PASSES, 4 * WIDTH], U8, align_bytes=64)
+        q_planes = keep.tile([P, PASSES, WIDTH], U8, align_bytes=64)
+        kv_planes = keep.tile([P, PASSES, 2 * WIDTH], U8, align_bytes=64)
         g_row = keep.tile([P, WIDTH], BF16)
-        g_all = keep.tile([P, WIDTH], F32)
+        g_all = keep.tile([P, WIDTH], BF16)
         ones = keep.tile([P, P], BF16)
         idle_rows = keep.tile([P, BANK], BF16)
         identity = keep.tile([P, P], F32)
         one = keep.tile([P, 1], F32)
         root_of_one = keep.tile([P, 1], F32)
-        statistics = keep.tile([P, TOKEN_TILES + 1, HEADS // 2, STATISTICS], F32)
-        squares = keep.tile([P, TOKEN_TILES + 1, HEADS], F32)
-        q_dots = keep.tile([P, TOKEN_TILES, HEADS], F32)
-        norms = keep.tile([P, TOKEN_TILES, HEADS], F32)
-        cosines = keep.tile([P, TOKEN_TILES, HEADS], F32)
-        sim_by_token = keep.tile([P, P], F32)
-        sim_by_tile = keep.tile([P, P], F32)
+        statistics = keep.tile([P, TILES + 1, HEADS // 2, STATISTICS], F32)
+        squares = keep.tile([P, TILES + 1, HEADS], F32)
+        q_dots = keep.tile([P, TILES, HEADS], F32)
+        norms = keep.tile([P, TILES, HEADS], F32)
+        cosines = keep.tile([P, TILES, HEADS], F32)
+        sim_by_token = keep.tile([P, 2, P], F32)
+        sim_rows = keep.tile([P, P, 2], F32)
 
+        nc.vector.memset(q_planes[:].bitcast(I32), 0)
         nc.vector.memset(ones[:], 1.0)
-        nc.vector.memset(idle_rows[:], 0.0)
-        nc.vector.memset(w_planes[:].bitcast(I32), 0)
-        nc.vector.memset(g_row[:], 0.0)
+        nc.vector.memset(idle_rows[:].bitcast(I32), 0)
+        nc.vector.memset(g_row[:].bitcast(I32), 0)
         nc.vector.memset(one[:], 1.0)
-        nc.vector.memset(sim_by_token[:], 0.0)
         masks.make_identity(nc, identity[:])
+        nc.gpsimd.memset(kv_planes[:].bitcast(I32), 0)
+        nc.gpsimd.memset(sim_by_token[:], 0.0)
         nc.scalar.activation(out=root_of_one[:], in_=one[:], func=ACT.Sqrt)
 
-        for j in range(TOKEN_TILES // 2):
-            nc.sync.dma_start(out=x_sb[:, 2 * j : 2 * j + 2, :], in_=x_pairs[j])
-        nc.sync.dma_start(out=g_row[0:1, :], in_=q_g.rearrange("(o h) d -> o (h d)", o=1))
-        for r in range(4):
+        def load_x(first, last):
             nc.sync.dma_start(
-                out=w_planes[r:P:32, :, :].bitcast(I32),
-                in_=w_scales[:, r:16:4, :].bitcast(I32).rearrange("g q n -> q g n"),
-            )
-        for c in range(QKV):
-            cols = slice(2 * WIDTH * c, 2 * WIDTH * (c + 1))
-            nc.sync.dma_start(
-                out=w_sb[:, c, :, :].bitcast(I32),
-                in_=w_words[:, :, cols].bitcast(I32).rearrange("g p n -> p g n"),
+                out=x_sb[:, 2 * first : 2 * last, :].rearrange("p (j i) k -> p j (i k)", i=2),
+                in_=x_pairs[:, first:last, :],
             )
 
-        def transpose_x(m):
+        def load_scales(planes, first, width, r):
+            nc.sync.dma_start(
+                out=planes[r:P:32, :, :].bitcast(I32),
+                in_=w_scales[:, r:16:4, first : first + width].bitcast(I32).rearrange("g q n -> q g n"),
+            )
+
+        def load_words(words, first, width):
+            nc.sync.dma_start(
+                out=words[:].bitcast(I32),
+                in_=w_words[:, :, 2 * first : 2 * (first + width)].bitcast(I32).rearrange("g p n -> p g n"),
+            )
+
+        load_x(0, 1)
+        load_scales(q_planes, 0, WIDTH, 0)
+        load_scales(q_planes, 0, WIDTH, 1)
+        nc.sync.dma_start(out=g_row[0:1, :], in_=q_g.rearrange("(o h) d -> o (h d)", o=1))
+        load_x(1, 2)
+        load_scales(q_planes, 0, WIDTH, 2)
+        load_scales(q_planes, 0, WIDTH, 3)
+        load_words(q_words, 0, WIDTH)
+        load_x(2, 4)
+        load_scales(kv_planes, WIDTH, 2 * WIDTH, 0)
+        load_words(kv_words, WIDTH, 2 * WIDTH)
+        load_scales(kv_planes, WIDTH, 2 * WIDTH, 1)
+
+        idle_product = banks.tile([P, BANK], F32, tag="bank")
+
+        def keep_the_clock_up(count):
+            for repeat in range(count):
+                nc.tensor.matmul(out=idle_product[:], lhsT=ones[:], rhs=idle_rows[:], start=True, stop=True)
+
+        def transpose_x(m, copy_out):
             words = x_sb[:, m, :].bitcast(F32)
             halves = banks.tile([P, PASSES, 2, P], F32, tag="bank")
             for g in range(PASSES):
@@ -102,7 +127,6 @@ def tile_memeffattention_pa_kernel(tc, x, w_words, w_scales, q_g, q_out, k_out, 
                         identity=identity[:],
                     )
             grouped = regroup.tile([P, K], BF16, align_bytes=64)
-            copy_out = nc.scalar.copy if m % 2 == 0 else nc.vector.tensor_copy
             copy_out(
                 out=grouped[:].bitcast(F32).rearrange("p (g r u) -> p g r u", g=PASSES, u=2),
                 in_=halves[:].rearrange("p g u r -> p g r u"),
@@ -112,121 +136,170 @@ def tile_memeffattention_pa_kernel(tc, x, w_words, w_scales, q_g, q_out, k_out, 
         def quantise_x(m, grouped):
             nc.vector.quantize_mx(out=x_codes[:, m, :].bitcast(FP8X4), scales=x_scales[:, m, :], in_=grouped[:])
 
-        def project(m, c, n):
+        def project(m, words, planes, col):
             product = banks.tile([P, BANK], F32, tag="bank")
-            plane_cols = slice(WIDTH * c + BANK * n, WIDTH * c + BANK * (n + 1))
             for g in range(PASSES):
                 nc.tensor.matmul_mx(
                     out=product[:],
                     lhsT=x_codes[:, m, P * g : P * (g + 1)].bitcast(FP8X4),
                     lhsT_scale=x_scales[:, m, P * g : P * (g + 1)],
-                    rhs=w_sb[:, c, g, 2 * BANK * n : 2 * BANK * (n + 1)].bitcast(FP4X4),
-                    rhs_scale=w_planes[:, g, plane_cols],
+                    rhs=words[:, g, 2 * col : 2 * (col + BANK)].bitcast(FP4X4),
+                    rhs_scale=planes[:, g, col : col + BANK],
                     start=(g == 0),
                     stop=(g == PASSES - 1),
                 )
             return product
 
-        def head_statistics(rows, row):
-            for pair in range(HEADS // 2):
+        def head_statistics(rows, row, pairs):
+            for pair in pairs:
                 nc.vector.bn_stats(
                     out=statistics[:, row, pair, :],
                     in_=rows[:, 2 * HEAD_DIM * pair : 2 * HEAD_DIM * (pair + 1)].rearrange("p (s d) -> p d s", s=2),
                 )
 
-        def q_part(m):
-            q_sb = results.tile([P, WIDTH], F32)
-            terms = scratch.tile([P, WIDTH], F32)
-            for n in range(BANKS_PER_OUTPUT):
-                cols = slice(BANK * n, BANK * (n + 1))
-                nc.scalar.copy(out=q_sb[:, cols], in_=project(m, 0, n)[:])
-                nc.gpsimd.tensor_tensor(out=terms[:, cols], in0=q_sb[:, cols], in1=g_all[:, cols], op=ALU.mult)
-            nc.sync.dma_start(out=q_tiles[m], in_=q_sb[:])
-            head_statistics(q_sb, m)
-            return terms
+        q_sb = []
+        terms_of = []
 
-        def dots_with_g(m, terms):
+        def q_part(m):
+            if m % 2 == 0:
+                q_pair = results.tile([P, 2, WIDTH], F32, tag="pair")
+                q_sb.append(q_pair)
+            rows = q_sb[m // 2][:, m % 2, :]
+            for n in range(HALVES):
+                nc.scalar.copy(out=rows[:, BANK * n : BANK * (n + 1)], in_=project(m, q_words, q_planes, BANK * n)[:])
+            terms = scratch.tile([P, WIDTH], F32)
+            nc.gpsimd.tensor_tensor(out=terms[:], in0=rows, in1=g_all[:], op=ALU.mult)
+            terms_of.append(terms)
+            if m % 2 == 1:
+                nc.sync.dma_start(out=q_pairs[m // 2], in_=q_sb[m // 2][:])
+
+        def statistics_of(m):
+            head_statistics(q_sb[m // 2][:, m % 2, :], m, range(HEADS // 2))
+
+        def dots_with_g(m):
             nc.vector.tensor_reduce(
-                out=q_dots[:, m, :], in_=terms[:].rearrange("p (h d) -> p h d", h=HEADS), axis=AXIS.X, op=ALU.add
+                out=q_dots[:, m, :], in_=terms_of[m][:].rearrange("p (h d) -> p h d", h=HEADS), axis=AXIS.X, op=ALU.add
             )
 
-        def k_part(m):
-            k_sb = results.tile([P, WIDTH], F32)
-            for n in range(BANKS_PER_OUTPUT):
-                nc.scalar.copy(out=k_sb[:, BANK * n : BANK * (n + 1)], in_=project(m, 1, n)[:])
-            nc.sync.dma_start(out=k_tiles[m], in_=k_sb[:])
-
-        def v_part(m):
-            v_sb = results.tile([P, WIDTH], F32)
-            at_the_end = m == TOKEN_TILES - 1
-            for n in range(BANKS_PER_OUTPUT):
-                cols = slice(BANK * n, BANK * (n + 1))
-                nc.scalar.copy(out=v_sb[:, cols], in_=project(m, 2, n)[:])
-                if at_the_end:
-                    nc.sync.dma_start(out=v_tiles[m][:, cols], in_=v_sb[:, cols])
-            if not at_the_end:
-                nc.sync.dma_start(out=v_tiles[m], in_=v_sb[:])
-
-        idle_product = banks.tile([P, BANK], F32, tag="bank")
-
-        def keep_the_clock_up(count):
-            for repeat in range(count):
-                nc.tensor.matmul(out=idle_product[:], lhsT=ones[:], rhs=idle_rows[:], start=True, stop=True)
-
         keep_the_clock_up(WARM_UP)
-        grouped = [transpose_x(0)]
-        keep_the_clock_up(1)
-        for m in range(1, TOKEN_TILES):
-            grouped.append(transpose_x(m))
-            keep_the_clock_up(1)
-            quantise_x(m - 1, grouped[m - 1])
-        quantise_x(TOKEN_TILES - 1, grouped[TOKEN_TILES - 1])
-
+        grouped = [transpose_x(0, nc.scalar.copy), transpose_x(1, nc.vector.tensor_copy)]
+        quantise_x(0, grouped[0])
         g_spread = banks.tile([P, WIDTH], BF16, tag="bank")
-        for n in range(BANKS_PER_OUTPUT):
+        for n in range(HALVES):
             cols = slice(BANK * n, BANK * (n + 1))
             nc.tensor.matmul(out=g_spread[:, cols], lhsT=ones[:], rhs=g_row[:, cols], start=True, stop=True)
+        grouped.append(transpose_x(2, nc.scalar.copy))
         nc.vector.tensor_copy(out=g_all[:], in_=g_spread[:])
-        head_statistics(g_all, TOKEN_TILES)
+        quantise_x(1, grouped[1])
+        grouped.append(transpose_x(3, nc.vector.tensor_copy))
+        keep_the_clock_up(2)
+        quantise_x(2, grouped[2])
+        head_statistics(g_all, TILES, range(HEADS // 2))
+        quantise_x(3, grouped[3])
 
-        terms_of_tile = []
-        for m in range(TOKEN_TILES):
-            terms_of_tile.append(q_part(m))
-            if m >= 1:
-                dots_with_g(m - 1, terms_of_tile[m - 1])
-            if m >= 2:
-                k_part(m - 2)
-                v_part(m - 2)
+        q_part(0)
+        q_part(1)
+        load_scales(kv_planes, WIDTH, 2 * WIDTH, 2)
+        statistics_of(0)
+        grouped.append(transpose_x(4, nc.scalar.copy))
+        grouped.append(transpose_x(5, nc.scalar.copy))
+        quantise_x(4, grouped[4])
+        q_part(2)
+        statistics_of(1)
+        quantise_x(5, grouped[5])
+        q_part(3)
+        load_scales(kv_planes, WIDTH, 2 * WIDTH, 3)
+        dots_with_g(0)
+        grouped.append(transpose_x(6, nc.scalar.copy))
+        grouped.append(transpose_x(7, nc.scalar.copy))
+        quantise_x(6, grouped[6])
+        q_part(4)
+        statistics_of(2)
+        quantise_x(7, grouped[7])
+        q_part(5)
+        statistics_of(3)
+        q_part(6)
+        dots_with_g(1)
+        q_part(7)
 
-        last = TOKEN_TILES - 1
-        dots_with_g(last, terms_of_tile[last])
-        by_head = statistics[:].rearrange("p m c (s t) -> p m (c s) t", s=2)
-        means = by_head[:, :, :, 1]
-        spreads = by_head[:, :, :, 2]
-        nc.vector.tensor_tensor(out=squares[:], in0=means, in1=means, op=ALU.mult)
-        nc.vector.scalar_tensor_tensor(
-            out=squares[:], in0=squares[:], scalar=float(HEAD_DIM), in1=spreads, op0=ALU.mult, op1=ALU.add
-        )
-        nc.vector.tensor_tensor(
-            out=norms[:],
-            in0=squares[:, 0:TOKEN_TILES, :],
-            in1=squares[:, TOKEN_TILES : TOKEN_TILES + 1, :].to_broadcast([P, TOKEN_TILES, HEADS]),
-            op=ALU.mult,
-        )
-        k_part(last - 1)
-        v_part(last - 1)
-        nc.scalar.activation(out=norms[:], in_=norms[:], func=ACT.Sqrt, scale=float(HEADS * HEADS))
-        nc.vector.reciprocal(out=norms[:], in_=norms[:])
-        nc.vector.tensor_tensor(out=cosines[:], in0=q_dots[:], in1=norms[:], op=ALU.mult)
-        nc.vector.tensor_reduce(out=sim_by_token[:, 0:TOKEN_TILES], in_=cosines[:], axis=AXIS.X, op=ALU.add)
-        k_part(last)
-        v_part(last)
-        sim_rows = banks.tile([P, P], F32, tag="bank")
-        nc.tensor.transpose(out=sim_rows[:], in_=sim_by_token[:], identity=identity[:])
-        nc.scalar.copy(out=sim_by_tile[0:16, :], in_=sim_rows[0:16, :])
-        first_row = P - REGISTER_TOKENS
-        nc.sync.dma_start(out=sim_out[0:1, 0:first_row], in_=sim_by_tile[0:1, REGISTER_TOKENS:P])
-        nc.sync.dma_start(
-            out=sim_out[0:1, first_row : TOKENS - REGISTER_TOKENS].rearrange("o (m p) -> (o m) p", p=P),
-            in_=sim_by_tile[1:TOKEN_TILES, :],
-        )
+        backlog = []
+        for m in range(4, TILES):
+            backlog.append((statistics_of, m))
+            backlog.append((dots_with_g, m - 2))
+        for m in range(TILES - 2, TILES):
+            backlog.append((dots_with_g, m))
+
+        def work_off(unit):
+            for work, m in backlog[unit : unit + 1]:
+                work(m)
+
+        def norms_before_root():
+            by_head = statistics[:].rearrange("p m c (s t) -> p m (c s) t", s=2)
+            means = by_head[:, :, :, 1]
+            spreads = by_head[:, :, :, 2]
+            nc.vector.tensor_tensor(out=squares[:], in0=means, in1=means, op=ALU.mult)
+            nc.vector.scalar_tensor_tensor(
+                out=squares[:], in0=squares[:], scalar=float(HEAD_DIM), in1=spreads, op0=ALU.mult, op1=ALU.add
+            )
+            nc.vector.tensor_tensor(
+                out=norms[:],
+                in0=squares[:, 0:TILES, :],
+                in1=squares[:, TILES : TILES + 1, :].to_broadcast([P, TILES, HEADS]),
+                op=ALU.mult,
+            )
+
+        def similarity():
+            nc.vector.tensor_tensor(out=cosines[:], in0=q_dots[:], in1=norms[:], op=ALU.mult)
+            nc.vector.tensor_reduce(
+                out=sim_by_token[:, :, 0:PAIRS],
+                in_=cosines[:].rearrange("p (j i) h -> p i j h", i=2),
+                axis=AXIS.X,
+                op=ALU.add,
+            )
+
+        def store_similarity():
+            rows = banks.tile([P, 2, P], F32, tag="bank")
+            for i in range(2):
+                nc.tensor.transpose(out=rows[:, i, :], in_=sim_by_token[:, i, :], identity=identity[:])
+            nc.scalar.copy(out=sim_rows[0:16, :, :], in_=rows[0:16, :, :].rearrange("j i p -> j p i"))
+            by_pair = sim_rows[:].rearrange("j p i -> j (p i)")
+            first_row = 2 * P - REGISTER_TOKENS
+            nc.sync.dma_start(out=sim_out[0:1, 0:first_row], in_=by_pair[0:1, REGISTER_TOKENS : 2 * P])
+            nc.sync.dma_start(
+                out=sim_out[0:1, first_row : TOKENS - REGISTER_TOKENS].rearrange("o (j t) -> (o j) t", t=2 * P),
+                in_=by_pair[1:PAIRS, :],
+            )
+
+        unit = 0
+        for j in range(PAIRS):
+            for c in range(2):
+                pair = results.tile([P, 2, WIDTH], F32, tag="pair")
+                out_pairs = (k_pairs, v_pairs)[c]
+                at_the_end = j == PAIRS - 1 and c == 1
+                for i in range(2):
+                    if unit == 15:
+                        store_similarity()
+                    on_vector = unit >= 12
+                    for n in range(HALVES):
+                        cols = slice(BANK * n, BANK * (n + 1))
+                        copy_out = nc.vector.tensor_copy if on_vector and n == 1 else nc.scalar.copy
+                        copy_out(
+                            out=pair[:, i, cols],
+                            in_=project(2 * j + i, kv_words, kv_planes, WIDTH * c + BANK * n)[:],
+                        )
+                        if at_the_end and i == 1:
+                            nc.sync.dma_start(out=out_pairs[j][:, i, cols], in_=pair[:, i, cols])
+                    if at_the_end and i == 0:
+                        nc.sync.dma_start(out=out_pairs[j][:, i, :], in_=pair[:, i, :])
+                    work_off(unit)
+                    if unit == 6:
+                        norms_before_root()
+                    if unit == 10:
+                        nc.scalar.activation(out=norms[:], in_=norms[:], func=ACT.Sqrt, scale=float(HEADS * HEADS))
+                    if unit == 10:
+                        nc.vector.reciprocal(out=norms[:], in_=norms[:])
+                    if unit == 12:
+                        similarity()
+                    unit += 1
+                if not at_the_end:
+                    nc.sync.dma_start(out=out_pairs[j], in_=pair[:])

@@ -277,16 +277,10 @@ def tile_memeffattention_pa_kernel(tc, x, w_words, w_scales, q_g, q_out, k_out, 
                 out_pairs = (k_pairs, v_pairs)[c]
                 at_the_end = j == PAIRS - 1 and c == 1
                 for i in range(2):
-                    if unit == 15:
-                        store_similarity()
-                    on_vector = unit >= 12
                     for n in range(HALVES):
                         cols = slice(BANK * n, BANK * (n + 1))
-                        copy_out = nc.vector.tensor_copy if on_vector and n == 1 else nc.scalar.copy
-                        copy_out(
-                            out=pair[:, i, cols],
-                            in_=project(2 * j + i, kv_words, kv_planes, WIDTH * c + BANK * n)[:],
-                        )
+                        product = project(2 * j + i, kv_words, kv_planes, WIDTH * c + BANK * n)
+                        nc.scalar.copy(out=pair[:, i, cols], in_=product[:])
                         if at_the_end and i == 1:
                             nc.sync.dma_start(out=out_pairs[j][:, i, cols], in_=pair[:, i, cols])
                     if at_the_end and i == 0:
@@ -303,3 +297,4 @@ def tile_memeffattention_pa_kernel(tc, x, w_words, w_scales, q_g, q_out, k_out, 
                     unit += 1
                 if not at_the_end:
                     nc.sync.dma_start(out=out_pairs[j], in_=pair[:])
+        store_similarity()

@@ -200,23 +200,21 @@ def tile_memeffattention_pa_kernel(tc, x, w_words, w_scales, q_g, q_out, k_out, 
         q_part(0)
         q_part(1)
         load_scales(kv_planes, WIDTH, 2 * WIDTH, 2)
-        statistics_of(0)
-        grouped.append(transpose_x(4, nc.scalar.copy))
-        grouped.append(transpose_x(5, nc.scalar.copy))
+        for m in range(4, TILES):
+            grouped.append(transpose_x(m, nc.scalar.copy if m % 2 == 0 else nc.vector.tensor_copy))
         quantise_x(4, grouped[4])
-        q_part(2)
-        statistics_of(1)
+        statistics_of(0)
         quantise_x(5, grouped[5])
+        quantise_x(6, grouped[6])
+        quantise_x(7, grouped[7])
+        q_part(2)
         q_part(3)
         load_scales(kv_planes, WIDTH, 2 * WIDTH, 3)
-        dots_with_g(0)
-        grouped.append(transpose_x(6, nc.scalar.copy))
-        grouped.append(transpose_x(7, nc.scalar.copy))
-        quantise_x(6, grouped[6])
+        statistics_of(1)
         q_part(4)
         statistics_of(2)
-        quantise_x(7, grouped[7])
         q_part(5)
+        dots_with_g(0)
         statistics_of(3)
         q_part(6)
         dots_with_g(1)
@@ -281,9 +279,7 @@ def tile_memeffattention_pa_kernel(tc, x, w_words, w_scales, q_g, q_out, k_out, 
                         cols = slice(BANK * n, BANK * (n + 1))
                         product = project(2 * j + i, kv_words, kv_planes, WIDTH * c + BANK * n)
                         nc.scalar.copy(out=pair[:, i, cols], in_=product[:])
-                        if at_the_end and i == 1:
-                            nc.sync.dma_start(out=out_pairs[j][:, i, cols], in_=pair[:, i, cols])
-                    if at_the_end and i == 0:
+                    if at_the_end:
                         nc.sync.dma_start(out=out_pairs[j][:, i, :], in_=pair[:, i, :])
                     work_off(unit)
                     if unit == 6:

@@ -109,6 +109,7 @@ def tile_memeffattention_pa_kernel(tc, x, w_words, w_scales, q_g, q_out, k_out, 
         load_scales(kv_planes, WIDTH, 2 * WIDTH, 0)
         load_words(kv_words, WIDTH, 2 * WIDTH)
         load_scales(kv_planes, WIDTH, 2 * WIDTH, 1)
+        load_scales(kv_planes, WIDTH, 2 * WIDTH, 2)
 
         idle_product = banks.tile([P, BANK], F32, tag="bank")
 
@@ -199,7 +200,7 @@ def tile_memeffattention_pa_kernel(tc, x, w_words, w_scales, q_g, q_out, k_out, 
 
         q_part(0)
         q_part(1)
-        load_scales(kv_planes, WIDTH, 2 * WIDTH, 2)
+        load_scales(kv_planes, WIDTH, 2 * WIDTH, 3)
         for m in range(4, TILES):
             grouped.append(transpose_x(m, nc.scalar.copy if m % 2 == 0 else nc.vector.tensor_copy))
         quantise_x(4, grouped[4])
@@ -209,7 +210,6 @@ def tile_memeffattention_pa_kernel(tc, x, w_words, w_scales, q_g, q_out, k_out, 
         quantise_x(7, grouped[7])
         q_part(2)
         q_part(3)
-        load_scales(kv_planes, WIDTH, 2 * WIDTH, 3)
         statistics_of(1)
         q_part(4)
         statistics_of(2)

@@ -171,8 +171,7 @@ def tile_memeffattention_pa_kernel(tc, x, w_words, w_scales, q_g, q_out, k_out, 
             terms = scratch.tile([P, WIDTH], F32)
             nc.gpsimd.tensor_tensor(out=terms[:], in0=rows, in1=g_all[:], op=ALU.mult)
             terms_of.append(terms)
-            if m % 2 == 1:
-                nc.sync.dma_start(out=q_pairs[m // 2], in_=q_sb[m // 2][:])
+            nc.sync.dma_start(out=q_pairs[m // 2][:, m % 2, :], in_=rows)
 
         def statistics_of(m):
             head_statistics(q_sb[m // 2][:, m % 2, :], m, range(HEADS // 2))
@@ -201,15 +200,15 @@ def tile_memeffattention_pa_kernel(tc, x, w_words, w_scales, q_g, q_out, k_out, 
         q_part(0)
         q_part(1)
         load_scales(kv_planes, WIDTH, 2 * WIDTH, 3)
+        statistics_of(0)
+        q_part(2)
         for m in range(4, TILES):
             grouped.append(transpose_x(m, nc.scalar.copy if m % 2 == 0 else nc.vector.tensor_copy))
-        quantise_x(4, grouped[4])
-        statistics_of(0)
-        quantise_x(5, grouped[5])
-        quantise_x(6, grouped[6])
-        quantise_x(7, grouped[7])
-        q_part(2)
+            if m % 2 == 1:
+                quantise_x(m - 1, grouped[m - 1])
         q_part(3)
+        quantise_x(5, grouped[5])
+        quantise_x(7, grouped[7])
         statistics_of(1)
         q_part(4)
         statistics_of(2)
@@ -273,14 +272,12 @@ def tile_memeffattention_pa_kernel(tc, x, w_words, w_scales, q_g, q_out, k_out, 
             for c in range(2):
                 pair = results.tile([P, 2, WIDTH], F32, tag="pair")
                 out_pairs = (k_pairs, v_pairs)[c]
-                at_the_end = j == PAIRS - 1 and c == 1
                 for i in range(2):
                     for n in range(HALVES):
                         cols = slice(BANK * n, BANK * (n + 1))
                         product = project(2 * j + i, kv_words, kv_planes, WIDTH * c + BANK * n)
                         nc.scalar.copy(out=pair[:, i, cols], in_=product[:])
-                    if at_the_end:
-                        nc.sync.dma_start(out=out_pairs[j][:, i, :], in_=pair[:, i, :])
+                    nc.sync.dma_start(out=out_pairs[j][:, i, :], in_=pair[:, i, :])
                     work_off(unit)
                     if unit == 6:
                         norms_before_root()
@@ -291,6 +288,4 @@ def tile_memeffattention_pa_kernel(tc, x, w_words, w_scales, q_g, q_out, k_out, 
                     if unit == 12:
                         similarity()
                     unit += 1
-                if not at_the_end:
-                    nc.sync.dma_start(out=out_pairs[j], in_=pair[:])
         store_similarity()

@@ -27,7 +27,7 @@ PASSES = K // (4 * P)
 BANK = 512
 HALVES = WIDTH // BANK
 STATISTICS = 6
-WARM_UP = 4
+WARM_UP = 3
 
 FLOPS = 2 * TOKENS * K * 3 * WIDTH
 
@@ -48,6 +48,7 @@ def tile_memeffattention_pa_kernel(tc, x, w_words, w_scales, q_g, q_out, k_out, 
         ctx.enter_context(tc.manual_schedule())
 
         x_sb = keep.tile([P, TILES, K], BF16)
+        x_ordered = keep.tile([P, TILES // 2, K // 2], F32)
         x_codes = keep.tile([P, TILES, PASSES * P], U32, align_bytes=64)
         x_scales = keep.tile([P, TILES, PASSES * P], U8, align_bytes=64)
         q_words = keep.tile([P, PASSES, 2 * WIDTH], U8, align_bytes=64)
@@ -100,10 +101,10 @@ def tile_memeffattention_pa_kernel(tc, x, w_words, w_scales, q_g, q_out, k_out, 
         load_x(0, 1)
         load_scales(q_planes, 0, WIDTH, 0)
         load_scales(q_planes, 0, WIDTH, 1)
-        nc.sync.dma_start(out=g_row[0:1, :], in_=q_g.rearrange("(o h) d -> o (h d)", o=1))
         load_x(1, 2)
         load_scales(q_planes, 0, WIDTH, 2)
         load_scales(q_planes, 0, WIDTH, 3)
+        nc.sync.dma_start(out=g_row[0:1, :], in_=q_g.rearrange("(o h) d -> o (h d)", o=1))
         load_words(q_words, 0, WIDTH)
         load_x(2, 4)
         load_scales(kv_planes, WIDTH, 2 * WIDTH, 0)
@@ -122,17 +123,23 @@ def tile_memeffattention_pa_kernel(tc, x, w_words, w_scales, q_g, q_out, k_out, 
             halves = banks.tile([P, PASSES, 2, P], F32, tag="bank")
             for g in range(PASSES):
                 for u in range(2):
-                    nc.tensor.transpose(
-                        out=halves[:, g, u, :],
-                        in_=words[:, 2 * P * g + u : 2 * P * (g + 1) : 2],
-                        identity=identity[:],
-                    )
+                    if m < TILES // 2:
+                        half = words[:, 2 * P * g + u : 2 * P * (g + 1) : 2]
+                    else:
+                        half = x_ordered[:, m - TILES // 2, P * (2 * g + u) : P * (2 * g + u + 1)]
+                    nc.tensor.transpose(out=halves[:, g, u, :], in_=half, identity=identity[:])
             grouped = regroup.tile([P, K], BF16, align_bytes=64)
             copy_out(
                 out=grouped[:].bitcast(F32).rearrange("p (g r u) -> p g r u", g=PASSES, u=2),
                 in_=halves[:].rearrange("p g u r -> p g r u"),
             )
             return grouped
+
+        def order_words(m):
+            nc.vector.tensor_copy(
+                out=x_ordered[:, m - TILES // 2, :].rearrange("p (g u r) -> p g u r", g=PASSES, u=2),
+                in_=x_sb[:, m, :].bitcast(F32).rearrange("p (g r u) -> p g u r", g=PASSES, u=2),
+            )
 
         def quantise_x(m, grouped):
             nc.vector.quantize_mx(out=x_codes[:, m, :].bitcast(FP8X4), scales=x_scales[:, m, :], in_=grouped[:])
@@ -173,8 +180,8 @@ def tile_memeffattention_pa_kernel(tc, x, w_words, w_scales, q_g, q_out, k_out, 
             terms_of.append(terms)
             nc.sync.dma_start(out=q_pairs[m // 2][:, m % 2, :], in_=rows)
 
-        def statistics_of(m):
-            head_statistics(q_sb[m // 2][:, m % 2, :], m, range(HEADS // 2))
+        def statistics_of(m, pairs=range(HEADS // 2)):
+            head_statistics(q_sb[m // 2][:, m % 2, :], m, pairs)
 
         def dots_with_g(m):
             nc.vector.tensor_reduce(
@@ -184,23 +191,23 @@ def tile_memeffattention_pa_kernel(tc, x, w_words, w_scales, q_g, q_out, k_out, 
         keep_the_clock_up(WARM_UP)
         grouped = [transpose_x(0, nc.scalar.copy), transpose_x(1, nc.vector.tensor_copy)]
         quantise_x(0, grouped[0])
+        grouped.append(transpose_x(2, nc.scalar.copy))
+        quantise_x(1, grouped[1])
+        grouped.append(transpose_x(3, nc.vector.tensor_copy))
         g_spread = banks.tile([P, WIDTH], BF16, tag="bank")
         for n in range(HALVES):
             cols = slice(BANK * n, BANK * (n + 1))
             nc.tensor.matmul(out=g_spread[:, cols], lhsT=ones[:], rhs=g_row[:, cols], start=True, stop=True)
-        grouped.append(transpose_x(2, nc.scalar.copy))
-        nc.vector.tensor_copy(out=g_all[:], in_=g_spread[:])
-        quantise_x(1, grouped[1])
-        grouped.append(transpose_x(3, nc.vector.tensor_copy))
-        keep_the_clock_up(2)
         quantise_x(2, grouped[2])
-        head_statistics(g_all, TILES, range(HEADS // 2))
+        nc.vector.tensor_copy(out=g_all[:], in_=g_spread[:])
         quantise_x(3, grouped[3])
 
         q_part(0)
         q_part(1)
         load_scales(kv_planes, WIDTH, 2 * WIDTH, 3)
-        statistics_of(0)
+        statistics_of(0, range(HEADS // 4))
+        for m in range(4, TILES):
+            order_words(m)
         q_part(2)
         for m in range(4, TILES):
             grouped.append(transpose_x(m, nc.scalar.copy if m % 2 == 0 else nc.vector.tensor_copy))
@@ -209,7 +216,9 @@ def tile_memeffattention_pa_kernel(tc, x, w_words, w_scales, q_g, q_out, k_out, 
         q_part(3)
         quantise_x(5, grouped[5])
         quantise_x(7, grouped[7])
+        statistics_of(0, range(HEADS // 4, HEADS // 2))
         statistics_of(1)
+        head_statistics(g_all, TILES, range(HEADS // 2))
         q_part(4)
         statistics_of(2)
         q_part(5)

@@ -27,7 +27,7 @@ PASSES = K // (4 * P)
 BANK = 512
 HALVES = WIDTH // BANK
 STATISTICS = 6
-WARM_UP = 3
+WARM_UP = 4
 
 FLOPS = 2 * TOKENS * K * 3 * WIDTH
 
@@ -56,7 +56,9 @@ def tile_memeffattention_pa_kernel(tc, x, w_words, w_scales, q_g, q_out, k_out, 
         q_planes = keep.tile([P, PASSES, WIDTH], U8, align_bytes=64)
         kv_planes = keep.tile([P, PASSES, 2 * WIDTH], U8, align_bytes=64)
         g_row = keep.tile([P, WIDTH], BF16)
+        g_early = keep.tile([P, WIDTH], BF16)
         g_all = keep.tile([P, WIDTH], BF16)
+        last_terms = keep.tile([P, WIDTH], F32)
         ones = keep.tile([P, P], BF16)
         idle_rows = keep.tile([P, BANK], BF16)
         identity = keep.tile([P, P], F32)
@@ -174,11 +176,17 @@ def tile_memeffattention_pa_kernel(tc, x, w_words, w_scales, q_g, q_out, k_out, 
                 q_sb.append(q_pair)
             rows = q_sb[m // 2][:, m % 2, :]
             for n in range(HALVES):
-                nc.scalar.copy(out=rows[:, BANK * n : BANK * (n + 1)], in_=project(m, q_words, q_planes, BANK * n)[:])
-            terms = scratch.tile([P, WIDTH], F32)
-            nc.gpsimd.tensor_tensor(out=terms[:], in0=rows, in1=g_all[:], op=ALU.mult)
-            terms_of.append(terms)
+                cols = slice(BANK * n, BANK * (n + 1))
+                product = project(m, q_words, q_planes, BANK * n)
+                nc.scalar.copy(out=rows[:, cols], in_=product[:])
+                if m == TILES - 1:
+                    nc.vector.tensor_tensor(out=last_terms[:, cols], in0=product[:], in1=g_all[:, cols], op=ALU.mult)
             nc.sync.dma_start(out=q_pairs[m // 2][:, m % 2, :], in_=rows)
+
+        def multiply_by_g(m):
+            terms = scratch.tile([P, WIDTH], F32)
+            nc.gpsimd.tensor_tensor(out=terms[:], in0=q_sb[m // 2][:, m % 2, :], in1=g_all[:], op=ALU.mult)
+            terms_of.append(terms)
 
         def statistics_of(m, pairs=range(HEADS // 2)):
             head_statistics(q_sb[m // 2][:, m % 2, :], m, pairs)
@@ -190,8 +198,10 @@ def tile_memeffattention_pa_kernel(tc, x, w_words, w_scales, q_g, q_out, k_out, 
 
         keep_the_clock_up(WARM_UP)
         grouped = [transpose_x(0, nc.scalar.copy), transpose_x(1, nc.vector.tensor_copy)]
+        keep_the_clock_up(2)
         quantise_x(0, grouped[0])
         grouped.append(transpose_x(2, nc.scalar.copy))
+        keep_the_clock_up(1)
         quantise_x(1, grouped[1])
         grouped.append(transpose_x(3, nc.vector.tensor_copy))
         g_spread = banks.tile([P, WIDTH], BF16, tag="bank")
@@ -199,13 +209,14 @@ def tile_memeffattention_pa_kernel(tc, x, w_words, w_scales, q_g, q_out, k_out, 
             cols = slice(BANK * n, BANK * (n + 1))
             nc.tensor.matmul(out=g_spread[:, cols], lhsT=ones[:], rhs=g_row[:, cols], start=True, stop=True)
         quantise_x(2, grouped[2])
-        nc.vector.tensor_copy(out=g_all[:], in_=g_spread[:])
+        nc.vector.tensor_copy(out=g_early[:], in_=g_spread[:])
         quantise_x(3, grouped[3])
+        head_statistics(g_early, TILES, range(HEADS // 2))
 
         q_part(0)
         q_part(1)
         load_scales(kv_planes, WIDTH, 2 * WIDTH, 3)
-        statistics_of(0, range(HEADS // 4))
+        statistics_of(0, range(1))
         for m in range(4, TILES):
             order_words(m)
         q_part(2)
@@ -216,30 +227,34 @@ def tile_memeffattention_pa_kernel(tc, x, w_words, w_scales, q_g, q_out, k_out, 
         q_part(3)
         quantise_x(5, grouped[5])
         quantise_x(7, grouped[7])
-        statistics_of(0, range(HEADS // 4, HEADS // 2))
+        nc.vector.tensor_copy(out=g_all[:], in_=g_early[:])
+        for m in range(4):
+            multiply_by_g(m)
+        statistics_of(0, range(1, HEADS // 2))
         statistics_of(1)
-        head_statistics(g_all, TILES, range(HEADS // 2))
         q_part(4)
+        multiply_by_g(4)
         statistics_of(2)
         q_part(5)
-        dots_with_g(0)
-        statistics_of(3)
+        multiply_by_g(5)
         q_part(6)
-        dots_with_g(1)
+        multiply_by_g(6)
         q_part(7)
+        terms_of.append(last_terms)
+        statistics_of(3)
 
-        backlog = []
+        backlog = [(dots_with_g, 0)]
         for m in range(4, TILES):
             backlog.append((statistics_of, m))
-            backlog.append((dots_with_g, m - 2))
-        for m in range(TILES - 2, TILES):
+            backlog.append((dots_with_g, m - 3))
+        for m in (TILES - 1, TILES - 3, TILES - 2):
             backlog.append((dots_with_g, m))
 
         def work_off(unit):
             for work, m in backlog[unit : unit + 1]:
                 work(m)
 
-        def norms_before_root():
+        def squared_norms():
             by_head = statistics[:].rearrange("p m c (s t) -> p m (c s) t", s=2)
             means = by_head[:, :, :, 1]
             spreads = by_head[:, :, :, 2]
@@ -253,8 +268,10 @@ def tile_memeffattention_pa_kernel(tc, x, w_words, w_scales, q_g, q_out, k_out, 
                 in1=squares[:, TILES : TILES + 1, :].to_broadcast([P, TILES, HEADS]),
                 op=ALU.mult,
             )
+            nc.vector.reciprocal(out=norms[:], in_=norms[:])
 
         def similarity():
+            nc.scalar.activation(out=norms[:], in_=norms[:], func=ACT.Sqrt, scale=1.0 / (HEADS * HEADS))
             nc.vector.tensor_tensor(out=cosines[:], in0=q_dots[:], in1=norms[:], op=ALU.mult)
             nc.vector.tensor_reduce(
                 out=sim_by_token[:, :, 0:PAIRS],
@@ -288,13 +305,9 @@ def tile_memeffattention_pa_kernel(tc, x, w_words, w_scales, q_g, q_out, k_out, 
                         nc.scalar.copy(out=pair[:, i, cols], in_=product[:])
                     nc.sync.dma_start(out=out_pairs[j][:, i, :], in_=pair[:, i, :])
                     work_off(unit)
-                    if unit == 6:
-                        norms_before_root()
-                    if unit == 10:
-                        nc.scalar.activation(out=norms[:], in_=norms[:], func=ACT.Sqrt, scale=float(HEADS * HEADS))
-                    if unit == 10:
-                        nc.vector.reciprocal(out=norms[:], in_=norms[:])
-                    if unit == 12:
+                    if unit == 9:
+                        squared_norms()
+                    if unit == 13:
                         similarity()
                     unit += 1
         store_similarity()

from contextlib import ExitStack

import concourse.masks as masks
import concourse.mybir as mybir

F32 = mybir.dt.float32
BF16 = mybir.dt.bfloat16
I32 = mybir.dt.int32
U32 = mybir.dt.uint32
U8 = mybir.dt.uint8
FP8X4 = mybir.dt.float8_e4m3fn_x4
FP4X4 = mybir.dt.float4_e2m1fn_x4
ACT = mybir.ActivationFunctionType
ALU = mybir.AluOpType
AXIS = mybir.AxisListType

P = 128
TOKENS = 1024
K = 1024
HEADS = 8
HEAD_DIM = 128
WIDTH = HEADS * HEAD_DIM
REGISTER_TOKENS = 5
TILES = TOKENS // P
PAIRS = TILES // 2
PASSES = K // (4 * P)
BANK = 512
HALVES = WIDTH // BANK
STATISTICS = 6
WARM_UP = 4

FLOPS = 2 * TOKENS * K * 3 * WIDTH


def tile_memeffattention_pa_kernel(tc, x, w_words, w_scales, q_g, q_out, k_out, v_out, sim_out):
    nc = tc.nc
    x_pairs = x.rearrange("b (j p i) k -> p (b j) (i k)", p=P, i=2)
    q_pairs = q_out.rearrange("b (j p i) h d -> (b j) p i (h d)", p=P, i=2)
    k_pairs = k_out.rearrange("b (j p i) h d -> (b j) p i (h d)", p=P, i=2)
    v_pairs = v_out.rearrange("b (j p i) h d -> (b j) p i (h d)", p=P, i=2)

    with ExitStack() as ctx:
        keep = ctx.enter_context(tc.tile_pool(name="keep", bufs=1))
        regroup = ctx.enter_context(tc.tile_pool(name="regroup", bufs=4))
        results = ctx.enter_context(tc.tile_pool(name="results", bufs=12))
        scratch = ctx.enter_context(tc.tile_pool(name="scratch", bufs=4))
        banks = ctx.enter_context(tc.psum_pool(name="banks", bufs=8))
        ctx.enter_context(tc.manual_schedule())

        x_sb = keep.tile([P, TILES, K], BF16)
        x_ordered = keep.tile([P, TILES // 2, K // 2], F32)
        x_codes = keep.tile([P, TILES, PASSES * P], U32, align_bytes=64)
        x_scales = keep.tile([P, TILES, PASSES * P], U8, align_bytes=64)
        q_words = keep.tile([P, PASSES, 2 * WIDTH], U8, align_bytes=64)
        kv_words = keep.tile([P, PASSES, 4 * WIDTH], U8, align_bytes=64)
        q_planes = keep.tile([P, PASSES, WIDTH], U8, align_bytes=64)
        kv_planes = keep.tile([P, PASSES, 2 * WIDTH], U8, align_bytes=64)
        g_row = keep.tile([P, WIDTH], BF16)
        g_early = keep.tile([P, WIDTH], BF16)
        g_all = keep.tile([P, WIDTH], BF16)
        last_terms = keep.tile([P, WIDTH], F32)
        ones = keep.tile([P, P], BF16)
        idle_rows = keep.tile([P, BANK], BF16)
        identity = keep.tile([P, P], F32)
        one = keep.tile([P, 1], F32)
        root_of_one = keep.tile([P, 1], F32)
        statistics = keep.tile([P, TILES + 1, HEADS // 2, STATISTICS], F32)
        squares = keep.tile([P, TILES + 1, HEADS], F32)
        q_dots = keep.tile([P, TILES, HEADS], F32)
        norms = keep.tile([P, TILES, HEADS], F32)
        cosines = keep.tile([P, TILES, HEADS], F32)
        sim_by_token = keep.tile([P, 2, P], F32)
        sim_rows = keep.tile([P, P, 2], F32)

        nc.vector.memset(q_planes[:].bitcast(I32), 0)
        nc.vector.memset(ones[:], 1.0)
        nc.vector.memset(idle_rows[:].bitcast(I32), 0)
        nc.vector.memset(g_row[:].bitcast(I32), 0)
        nc.vector.memset(one[:], 1.0)
        masks.make_identity(nc, identity[:])
        nc.gpsimd.memset(kv_planes[:].bitcast(I32), 0)
        nc.gpsimd.memset(sim_by_token[:], 0.0)
        nc.scalar.activation(out=root_of_one[:], in_=one[:], func=ACT.Sqrt)

        def load_x(first, last):
            nc.sync.dma_start(
                out=x_sb[:, 2 * first : 2 * last, :].rearrange("p (j i) k -> p j (i k)", i=2),
                in_=x_pairs[:, first:last, :],
            )

        def load_scales(planes, first, width, r):
            nc.sync.dma_start(
                out=planes[r:P:32, :, :].bitcast(I32),
                in_=w_scales[:, r:16:4, first : first + width].bitcast(I32).rearrange("g q n -> q g n"),
            )

        def load_words(words, first, width):
            nc.sync.dma_start(
                out=words[:].bitcast(I32),
                in_=w_words[:, :, 2 * first : 2 * (first + width)].bitcast(I32).rearrange("g p n -> p g n"),
            )

        load_x(0, 1)
        load_scales(q_planes, 0, WIDTH, 0)
        load_scales(q_planes, 0, WIDTH, 1)
        load_x(1, 2)
        load_scales(q_planes, 0, WIDTH, 2)
        load_scales(q_planes, 0, WIDTH, 3)
        nc.sync.dma_start(out=g_row[0:1, :], in_=q_g.rearrange("(o h) d -> o (h d)", o=1))
        load_words(q_words, 0, WIDTH)
        load_x(2, 4)
        load_scales(kv_planes, WIDTH, 2 * WIDTH, 0)
        load_words(kv_words, WIDTH, 2 * WIDTH)
        load_scales(kv_planes, WIDTH, 2 * WIDTH, 1)
        load_scales(kv_planes, WIDTH, 2 * WIDTH, 2)

        idle_product = banks.tile([P, BANK], F32, tag="bank")

        def keep_the_clock_up(count):
            for repeat in range(count):
                nc.tensor.matmul(out=idle_product[:], lhsT=ones[:], rhs=idle_rows[:], start=True, stop=True)

        def transpose_x(m, copy_out):
            words = x_sb[:, m, :].bitcast(F32)
            halves = banks.tile([P, PASSES, 2, P], F32, tag="bank")
            for g in range(PASSES):
                for u in range(2):
                    if m < TILES // 2:
                        half = words[:, 2 * P * g + u : 2 * P * (g + 1) : 2]
                    else:
                        half = x_ordered[:, m - TILES // 2, P * (2 * g + u) : P * (2 * g + u + 1)]
                    nc.tensor.transpose(out=halves[:, g, u, :], in_=half, identity=identity[:])
            grouped = regroup.tile([P, K], BF16, align_bytes=64)
            copy_out(
                out=grouped[:].bitcast(F32).rearrange("p (g r u) -> p g r u", g=PASSES, u=2),
                in_=halves[:].rearrange("p g u r -> p g r u"),
            )
            return grouped

        def order_words(m):
            nc.vector.tensor_copy(
                out=x_ordered[:, m - TILES // 2, :].rearrange("p (g u r) -> p g u r", g=PASSES, u=2),
                in_=x_sb[:, m, :].bitcast(F32).rearrange("p (g r u) -> p g u r", g=PASSES, u=2),
            )

        def quantise_x(m, grouped):
            nc.vector.quantize_mx(out=x_codes[:, m, :].bitcast(FP8X4), scales=x_scales[:, m, :], in_=grouped[:])

        def project(m, words, planes, col):
            product = banks.tile([P, BANK], F32, tag="bank")
            for g in range(PASSES):
                nc.tensor.matmul_mx(
                    out=product[:],
                    lhsT=x_codes[:, m, P * g : P * (g + 1)].bitcast(FP8X4),
                    lhsT_scale=x_scales[:, m, P * g : P * (g + 1)],
                    rhs=words[:, g, 2 * col : 2 * (col + BANK)].bitcast(FP4X4),
                    rhs_scale=planes[:, g, col : col + BANK],
                    start=(g == 0),
                    stop=(g == PASSES - 1),
                )
            return product

        def head_statistics(rows, row, pairs):
            for pair in pairs:
                nc.vector.bn_stats(
                    out=statistics[:, row, pair, :],
                    in_=rows[:, 2 * HEAD_DIM * pair : 2 * HEAD_DIM * (pair + 1)].rearrange("p (s d) -> p d s", s=2),
                )

        q_sb = []
        terms_of = []

        def q_part(m):
            if m % 2 == 0:
                q_pair = results.tile([P, 2, WIDTH], F32, tag="pair")
                q_sb.append(q_pair)
            rows = q_sb[m // 2][:, m % 2, :]
            for n in range(HALVES):
                cols = slice(BANK * n, BANK * (n + 1))
                product = project(m, q_words, q_planes, BANK * n)
                nc.scalar.copy(out=rows[:, cols], in_=product[:])
                if m == TILES - 1:
                    nc.vector.tensor_tensor(out=last_terms[:, cols], in0=product[:], in1=g_all[:, cols], op=ALU.mult)
            nc.sync.dma_start(out=q_pairs[m // 2][:, m % 2, :], in_=rows)

        def multiply_by_g(m):
            terms = scratch.tile([P, WIDTH], F32)
            nc.gpsimd.tensor_tensor(out=terms[:], in0=q_sb[m // 2][:, m % 2, :], in1=g_all[:], op=ALU.mult)
            terms_of.append(terms)

        def statistics_of(m, pairs=range(HEADS // 2)):
            head_statistics(q_sb[m // 2][:, m % 2, :], m, pairs)

        def dots_with_g(m):
            nc.vector.tensor_reduce(
                out=q_dots[:, m, :], in_=terms_of[m][:].rearrange("p (h d) -> p h d", h=HEADS), axis=AXIS.X, op=ALU.add
            )

        keep_the_clock_up(WARM_UP)
        grouped = [transpose_x(0, nc.scalar.copy), transpose_x(1, nc.vector.tensor_copy)]
        keep_the_clock_up(2)
        quantise_x(0, grouped[0])
        grouped.append(transpose_x(2, nc.scalar.copy))
        keep_the_clock_up(1)
        quantise_x(1, grouped[1])
        grouped.append(transpose_x(3, nc.vector.tensor_copy))
        g_spread = banks.tile([P, WIDTH], BF16, tag="bank")
        for n in range(HALVES):
            cols = slice(BANK * n, BANK * (n + 1))
            nc.tensor.matmul(out=g_spread[:, cols], lhsT=ones[:], rhs=g_row[:, cols], start=True, stop=True)
        quantise_x(2, grouped[2])
        nc.vector.tensor_copy(out=g_early[:], in_=g_spread[:])
        quantise_x(3, grouped[3])
        head_statistics(g_early, TILES, range(HEADS // 2))

        q_part(0)
        q_part(1)
        load_scales(kv_planes, WIDTH, 2 * WIDTH, 3)
        statistics_of(0, range(1))
        for m in range(4, TILES):
            order_words(m)
        q_part(2)
        for m in range(4, TILES):
            grouped.append(transpose_x(m, nc.scalar.copy if m % 2 == 0 else nc.vector.tensor_copy))
            if m % 2 == 1:
                quantise_x(m - 1, grouped[m - 1])
        q_part(3)
        quantise_x(5, grouped[5])
        quantise_x(7, grouped[7])
        nc.vector.tensor_copy(out=g_all[:], in_=g_early[:])
        for m in range(4):
            multiply_by_g(m)
        statistics_of(0, range(1, HEADS // 2))
        statistics_of(1)
        q_part(4)
        multiply_by_g(4)
        statistics_of(2)
        q_part(5)
        multiply_by_g(5)
        q_part(6)
        multiply_by_g(6)
        q_part(7)
        terms_of.append(last_terms)
        statistics_of(3)

        backlog = [(dots_with_g, 0)]
        for m in range(4, TILES):
            backlog.append((statistics_of, m))
            backlog.append((dots_with_g, m - 3))
        for m in (TILES - 1, TILES - 3, TILES - 2):
            backlog.append((dots_with_g, m))

        def work_off(unit):
            for work, m in backlog[unit : unit + 1]:
                work(m)

        def squared_norms():
            by_head = statistics[:].rearrange("p m c (s t) -> p m (c s) t", s=2)
            means = by_head[:, :, :, 1]
            spreads = by_head[:, :, :, 2]
            nc.vector.tensor_tensor(out=squares[:], in0=means, in1=means, op=ALU.mult)
            nc.vector.scalar_tensor_tensor(
                out=squares[:], in0=squares[:], scalar=float(HEAD_DIM), in1=spreads, op0=ALU.mult, op1=ALU.add
            )
            nc.vector.tensor_tensor(
                out=norms[:],
                in0=squares[:, 0:TILES, :],
                in1=squares[:, TILES : TILES + 1, :].to_broadcast([P, TILES, HEADS]),
                op=ALU.mult,
            )
            nc.vector.reciprocal(out=norms[:], in_=norms[:])

        def similarity():
            nc.scalar.activation(out=norms[:], in_=norms[:], func=ACT.Sqrt, scale=1.0 / (HEADS * HEADS))
            nc.vector.tensor_tensor(out=cosines[:], in0=q_dots[:], in1=norms[:], op=ALU.mult)
            nc.vector.tensor_reduce(
                out=sim_by_token[:, :, 0:PAIRS],
                in_=cosines[:].rearrange("p (j i) h -> p i j h", i=2),
                axis=AXIS.X,
                op=ALU.add,
            )

        def store_similarity():
            rows = banks.tile([P, 2, P], F32, tag="bank")
            for i in range(2):
                nc.tensor.transpose(out=rows[:, i, :], in_=sim_by_token[:, i, :], identity=identity[:])
            nc.scalar.copy(out=sim_rows[0:16, :, :], in_=rows[0:16, :, :].rearrange("j i p -> j p i"))
            by_pair = sim_rows[:].rearrange("j p i -> j (p i)")
            first_row = 2 * P - REGISTER_TOKENS
            nc.sync.dma_start(out=sim_out[0:1, 0:first_row], in_=by_pair[0:1, REGISTER_TOKENS : 2 * P])
            nc.sync.dma_start(
                out=sim_out[0:1, first_row : TOKENS - REGISTER_TOKENS].rearrange("o (j t) -> (o j) t", t=2 * P),
                in_=by_pair[1:PAIRS, :],
            )

        unit = 0
        for j in range(PAIRS):
            for c in range(2):
                pair = results.tile([P, 2, WIDTH], F32, tag="pair")
                out_pairs = (k_pairs, v_pairs)[c]
                for i in range(2):
                    for n in range(HALVES):
                        cols = slice(BANK * n, BANK * (n + 1))
                        product = project(2 * j + i, kv_words, kv_planes, WIDTH * c + BANK * n)
                        nc.scalar.copy(out=pair[:, i, cols], in_=product[:])
                    nc.sync.dma_start(out=out_pairs[j][:, i, :], in_=pair[:, i, :])
                    work_off(unit)
                    if unit == 9:
                        squared_norms()
                    if unit == 13:
                        similarity()
                    unit += 1
        store_similarity()
